import numpy as np
import ml_dtypes


def mxq(x, axis, fmt="e4m3"):
    dtype, down = {"e4m3": (ml_dtypes.float8_e4m3fn, 7), "e5m2": (ml_dtypes.float8_e5m2, 14)}[fmt]
    v = np.moveaxis(np.asarray(x, np.float32).astype(ml_dtypes.bfloat16).astype(np.float64), axis, -1)
    blocks = v.reshape(v.shape[:-1] + (-1, 32))
    amax = np.abs(blocks).max(-1, keepdims=True)
    byte = np.maximum(np.where(amax > 0, np.frexp(amax)[1] - 1 + 127, 0) - down, 1)
    scale = np.exp2(byte - 127.0)
    codes = (blocks / scale).astype(np.float32).astype(dtype).astype(np.float64)
    return np.moveaxis((codes * scale).reshape(v.shape), -1, axis)


WIDE = False


def mx_kscale(k):
    if not WIDE:
        return np.ones(k)
    levels = np.array([10, -10, 5, -5, 0])
    a = np.random.permutation(np.resize(levels, k // 512 * 4)).reshape(k // 512, 4)
    idx = np.arange(k)
    return np.exp2(a[idx // 512, idx % 128 // 32])


BF16 = ml_dtypes.bfloat16


def bf(x):
    return np.asarray(x, np.float32).astype(BF16)


def f64(x):
    return np.asarray(x).astype(np.float64)


E2M1 = np.array([0.0, 0.5, 1.0, 1.5, 2.0, 3.0, 4.0, 6.0, -0.0, -0.5, -1.0, -1.5, -2.0, -3.0, -4.0, -6.0])


def pack_weight(w, fmt):
    k, n = w.shape
    w = f64(bf(w)).reshape(k // 32, 32, n)
    amax = np.abs(w).max(1)
    if fmt == "e4m3":
        byte = np.frexp(amax)[1] - 1 + 127 - 7
    else:
        mant, ex = np.frexp(amax / 6.0)
        byte = np.where(mant > 0.5, ex, ex - 1) + 127
    byte = np.clip(np.where(amax > 0, byte, 1), 1, 254)
    scaled = (w * np.exp2(127.0 - byte)[:, None, :]).reshape(k, n).astype(np.float32)
    by_word = np.ascontiguousarray(scaled.reshape(k // 512, 128, 4, n).transpose(0, 1, 3, 2))
    if fmt == "e4m3":
        words = by_word.astype(ml_dtypes.float8_e4m3fn).view(np.uint8)
    else:
        c = by_word.astype(ml_dtypes.float4_e2m1fn).view(np.uint8) & 0xF
        words = c[..., 0::2] | (c[..., 1::2] << 4)
    return np.ascontiguousarray(words), np.ascontiguousarray(byte.astype(np.uint8).reshape(k // 512, 16, n))


def unpack_weight(words, scales, fmt):
    g, p, n, _ = words.shape
    if fmt == "e4m3":
        vals = np.ascontiguousarray(words).view(ml_dtypes.float8_e4m3fn).astype(np.float64)
    else:
        nib = np.empty((g, p, n, 4), np.uint8)
        nib[..., 0::2] = words & 0xF
        nib[..., 1::2] = words >> 4
        vals = E2M1[nib]
    vals = vals * np.repeat(np.exp2(scales.astype(np.float64) - 127.0), 8, axis=1)[..., None]
    return vals.transpose(0, 1, 3, 2).reshape(g * 512, n)


B, S, D, NH, HD, HID = 4, 256, 768, 4, 256, 1024


def setup_inputs():
    t = mx_kscale(HID)
    lengths = np.random.randint(S // 2, S + 1, size=B)
    tail = 0.05 + 0.45 * np.random.random_sample((B, S))
    mask = np.where(np.arange(S)[None, :] < lengths[:, None], 1.0, tail)
    h = np.random.standard_normal((NH, B, S, HD)) + 0.3 * np.random.standard_normal((NH, 1, 1, HD))
    W1 = bf(np.random.standard_normal((NH, HID, HD)) / np.sqrt(HD) * t[None, :, None])
    b1 = bf(np.random.standard_normal((NH, HID)) * 0.2 * t[None, :])
    W2 = np.random.standard_normal((NH, HD, HID)) * 2.5 / np.sqrt(HID) / t[None, None, :]
    cat = np.ascontiguousarray(W2.swapaxes(1, 2)).reshape(-1, HD)
    W2_words, W2_scales = pack_weight(cat, "e4m3")
    return {"h_heads": bf(h),
            "attention_mask": bf(mask),
            "W1": W1,
            "b1": b1,
            "W2_words": W2_words,
            "W2_scales": W2_scales}


def reference(h_heads, attention_mask, W1, b1, W2_words, W2_scales):
    h = f64(h_heads)
    pre = h.reshape(NH, B * S, HD) @ f64(W1).transpose(0, 2, 1) + f64(b1)[:, None, :]
    hid = np.maximum(pre, 0.0)
    a = mxq(hid, 2, "e4m3") @ unpack_weight(W2_words, W2_scales, "e4m3").reshape(NH, HID, HD)
    with np.errstate(divide="ignore"):
        log_mask = np.log(f64(attention_mask))[None, :, :, None]
    a = a.reshape(NH, B, S, HD) + log_mask
    e = np.exp(a - a.max(axis=2, keepdims=True))
    w = e / e.sum(axis=2, keepdims=True)
    v = (h * w).sum(axis=2)
    return v.transpose(1, 0, 2).reshape(B, NH * HD)

@@ -1,0 +1,235 @@
+from contextlib import ExitStack
+
+import concourse.mybir as mybir
+from concourse.masks import make_identity
+
+BF16 = mybir.dt.bfloat16
+F32 = mybir.dt.float32
+I32 = mybir.dt.int32
+U32 = mybir.dt.uint32
+U8 = mybir.dt.uint8
+FP8X4 = mybir.dt.float8_e4m3fn_x4
+ACT = mybir.ActivationFunctionType
+ALU = mybir.AluOpType
+AXIS = mybir.AxisListType
+
+P = 128
+NH, B, S, HD, HID = 4, 4, 256, 256, 1024
+PACK = 4
+K_PASS = P * PACK
+PASSES = HID // K_PASS
+F_TILES = HD // P
+TOKENS = B * S
+CHUNK = 512
+CHUNKS = TOKENS // CHUNK
+SENTENCES = CHUNK // S
+BLOCKS = CHUNK // P
+
+FLOPS = 2 * 2 * NH * TOKENS * HID * HD
+
+
+def tile_multiheadgeneralizedpooling_pa_e_kernel(
+    tc, h_heads, attention_mask, W1, b1, W2_words, W2_scales, out
+):
+    nc = tc.nc
+    with ExitStack() as ctx:
+        keep = ctx.enter_context(tc.tile_pool(name="keep", bufs=1))
+        hid_pool = ctx.enter_context(tc.tile_pool(name="hid", bufs=3))
+        soft_pool = ctx.enter_context(tc.tile_pool(name="soft", bufs=4))
+        psum_tp = ctx.enter_context(tc.psum_pool(name="psum_tp", bufs=2))
+        psum_pre = ctx.enter_context(tc.psum_pool(name="psum_pre", bufs=4))
+        psum_att = ctx.enter_context(tc.psum_pool(name="psum_att", bufs=2))
+
+        h_sb = keep.tile([P, NH, TOKENS // P, HD], BF16)
+        w1_sb = keep.tile([P, NH, PASSES, PACK, HD], BF16)
+        hT = keep.tile([P, NH, F_TILES, TOKENS], BF16)
+        w1T = keep.tile([P, NH, F_TILES, PASSES, PACK, P], BF16)
+        bias = keep.tile([P, NH, PASSES, PACK], BF16)
+        w2_words = keep.tile([P, NH * PASSES, HD], U32, align_bytes=64)
+        w2_scales = keep.tile([P, NH * PASSES, HD], U8, align_bytes=64)
+        mask_all = keep.tile([P, TOKENS], BF16)
+        log_mask = keep.tile([P, TOKENS], F32)
+        ident_bf = keep.tile([P, P], BF16)
+        ident_f32 = keep.tile([P, P], F32)
+        den = keep.tile([P, B * NH * F_TILES], F32)
+        num = keep.tile([P, B * NH * F_TILES], F32)
+        pooled = keep.tile([P, P], F32)
+
+        make_identity(nc, ident_bf[:])
+        make_identity(nc, ident_f32[:])
+        nc.vector.memset(w2_scales[:].rearrange("p g n -> p (g n)").bitcast(I32), 0)
+        nc.vector.memset(pooled[:], 0.0)
+
+        def load_w1(i, g):
+            rows = W1[i].rearrange("(g p t) f -> p g t f", g=PASSES, p=P, t=PACK)
+            nc.sync.dma_start(out=w1_sb[:, i, g], in_=rows[:, g])
+
+        def load_h(i, n):
+            rows = h_heads[i].flatten_outer_dims().rearrange("(j p) f -> p j f", p=P)
+            blocks = slice(n * BLOCKS, (n + 1) * BLOCKS)
+            nc.sync.dma_start(out=h_sb[:, i, blocks], in_=rows[:, blocks])
+
+        def load_w2_words(i):
+            groups = slice(i * PASSES, (i + 1) * PASSES)
+            words = W2_words.rearrange("g p n t -> g p (n t)").bitcast(I32)
+            nc.sync.dma_start(
+                out=w2_words[:, groups, :].bitcast(I32),
+                in_=words[groups].rearrange("g p n -> p g n"),
+            )
+
+        nc.scalar.dma_start(
+            out=bias[:], in_=b1.rearrange("i (g p t) -> p i g t", g=PASSES, p=P, t=PACK)
+        )
+        nc.scalar.dma_start(
+            out=mask_all[:], in_=attention_mask.rearrange("b s -> (b s)").partition_broadcast(P)
+        )
+        load_w1(0, 0)
+        load_h(0, 0)
+        load_w1(0, 1)
+        load_h(0, 1)
+        for quadrant in range(4):
+            nc.sync.dma_start(
+                out=w2_scales[32 * quadrant : 32 * quadrant + 4, :, :].bitcast(I32),
+                in_=W2_scales.bitcast(I32)[:, 4 * quadrant : 4 * quadrant + 4, :].rearrange(
+                    "g r n -> r g n"
+                ),
+            )
+        load_w2_words(0)
+        for i in range(1, NH):
+            load_w1(i, 0)
+            load_w1(i, 1)
+            load_h(i, 0)
+            load_h(i, 1)
+            load_w2_words(i)
+
+        nc.scalar.activation(out=log_mask[:], in_=mask_all[:], func=ACT.Ln)
+
+        def transpose_w1(i, g):
+            tp = psum_tp.tile([P, F_TILES, PACK, P], BF16, tag="tp")
+            for c in range(F_TILES):
+                for t in range(PACK):
+                    nc.tensor.transpose(
+                        tp[:, c, t, :], w1_sb[:, i, g, t, c * P : (c + 1) * P], ident_bf[:]
+                    )
+            nc.scalar.copy(out=w1T[:, i, :, g], in_=tp[:])
+
+        def transpose_h(i, n):
+            tp = psum_tp.tile([P, F_TILES, BLOCKS, P], BF16, tag="tp")
+            for c in range(F_TILES):
+                for j in range(BLOCKS):
+                    nc.tensor.transpose(
+                        tp[:, c, j, :], h_sb[:, i, n * BLOCKS + j, c * P : (c + 1) * P], ident_bf[:]
+                    )
+            nc.scalar.copy(
+                out=hT[:, i, :, n * CHUNK : (n + 1) * CHUNK],
+                in_=tp[:].rearrange("p c j t -> p c (j t)"),
+            )
+
+        def hidden_group(i, n, g, att):
+            tokens = slice(n * CHUNK, (n + 1) * CHUNK)
+            by_t = hid_pool.tile([P, PACK, CHUNK], BF16, tag="by_t")
+            for t in range(PACK):
+                pre = psum_pre.tile([P, CHUNK], F32, tag="pre")
+                for c in range(F_TILES):
+                    nc.tensor.matmul(
+                        pre[:],
+                        lhsT=w1T[:, i, c, g, t, :],
+                        rhs=hT[:, i, c, tokens],
+                        start=(c == 0),
+                        stop=(c == F_TILES - 1),
+                    )
+                nc.scalar.activation(
+                    out=by_t[:, t, :],
+                    in_=pre[:],
+                    func=ACT.Relu,
+                    bias=bias[:, i, g, t : t + 1],
+                    scale=1.0,
+                )
+            grouped = hid_pool.tile([P, CHUNK, PACK], BF16, tag="grouped", align_bytes=64)
+            nc.vector.tensor_copy(
+                out=grouped[:].rearrange("p (w r) t -> p w t r", r=4),
+                in_=by_t[:].rearrange("p t (w r) -> p w t r", r=4),
+            )
+            codes = hid_pool.tile([P, CHUNK], U32, tag="codes", align_bytes=64)
+            scales = hid_pool.tile([P, CHUNK], U8, tag="scales", align_bytes=64)
+            nc.vector.quantize_mx(
+                out=codes[:].bitcast(FP8X4),
+                scales=scales[:],
+                in_=grouped[:].rearrange("p w t -> p (w t)"),
+            )
+            group = i * PASSES + g
+            for m in range(F_TILES):
+                features = slice(m * P, (m + 1) * P)
+                nc.tensor.matmul_mx(
+                    out=att[m][:],
+                    lhsT=w2_words[:, group, features].bitcast(FP8X4),
+                    lhsT_scale=w2_scales[:, group, features],
+                    rhs=codes[:].bitcast(FP8X4),
+                    rhs_scale=scales[:],
+                    start=(g == 0),
+                    stop=(g == PASSES - 1),
+                )
+
+        def pool_chunk(i, n, att):
+            for m in range(F_TILES):
+                score = soft_pool.tile([P, SENTENCES, S], F32, tag="score")
+                nc.vector.tensor_tensor(
+                    out=score[:].rearrange("p b s -> p (b s)"),
+                    in0=att[m][:],
+                    in1=log_mask[:, n * CHUNK : (n + 1) * CHUNK],
+                    op=ALU.add,
+                )
+                neg_max = soft_pool.tile([P, SENTENCES], F32, tag="neg_max")
+                nc.vector.tensor_reduce(
+                    out=neg_max[:], in_=score[:], axis=AXIS.X, op=ALU.max, negate=True
+                )
+                for s in range(SENTENCES):
+                    sentence = n * SENTENCES + s
+                    column = (sentence * NH + i) * F_TILES + m
+                    weight = soft_pool.tile([P, S], F32, tag="weight")
+                    nc.scalar.activation(
+                        out=weight[:],
+                        in_=score[:, s, :],
+                        func=ACT.Exp,
+                        bias=neg_max[:, s : s + 1],
+                        scale=1.0,
+                        accum_out=den[:, column : column + 1],
+                    )
+                    weighted = soft_pool.tile([P, S], F32, tag="weighted")
+                    nc.vector.scalar_tensor_tensor(
+                        out=weighted[:],
+                        in0=weight[:],
+                        scalar=1.0,
+                        in1=hT[:, i, m, sentence * S : (sentence + 1) * S],
+                        op0=ALU.mult,
+                        op1=ALU.mult,
+                        accum_out=num[:, column : column + 1],
+                    )
+
+        transpose_w1(0, 0)
+        transpose_h(0, 0)
+        transpose_w1(0, 1)
+        transpose_h(0, 1)
+        for i in range(NH):
+            for n in range(CHUNKS):
+                att = [
+                    psum_att.tile([P, CHUNK], F32, name="att%d" % m, tag="att")
+                    for m in range(F_TILES)
+                ]
+                for g in range(PASSES):
+                    hidden_group(i, n, g, att)
+                    if i + 1 < NH and n == 0:
+                        transpose_w1(i + 1, g)
+                    if i + 1 < NH and n == 1:
+                        transpose_h(i + 1, g)
+                pool_chunk(i, n, att)
+
+        columns = B * NH * F_TILES
+        inv_den = keep.tile([P, columns], F32)
+        nc.vector.reciprocal(out=inv_den[:], in_=den[:])
+        nc.vector.tensor_mul(out=pooled[:, 0:columns], in0=num[:], in1=inv_den[:])
+        pooledT = psum_tp.tile([P, P], F32, tag="tp")
+        nc.tensor.transpose(pooledT[:], pooled[:], ident_f32[:])
+        result = keep.tile([columns, P], F32)
+        nc.vector.tensor_copy(out=result[:], in_=pooledT[0:columns, :])
+        nc.sync.dma_start(out=out.rearrange("b (r f) -> (b r) f", f=P), in_=result[:])

@@ -25,6 +25,11 @@ CHUNKS = TOKENS // CHUNK
 SENTENCES = CHUNK // S
 BLOCKS = CHUNK // P
 
+GROUPS = NH * CHUNKS * PASSES
+HALVES = NH * CHUNKS * F_TILES
+QUARTERS = NH * 4
+FIRST_QUARTERS = 3
+
 FLOPS = 2 * 2 * NH * TOKENS * HID * HD
 
 
@@ -33,16 +38,17 @@ def tile_multiheadgeneralizedpooling_pa_e_kernel(
 ):
     nc = tc.nc
     with ExitStack() as ctx:
+        ctx.enter_context(tc.manual_schedule())
         keep = ctx.enter_context(tc.tile_pool(name="keep", bufs=1))
         hid_pool = ctx.enter_context(tc.tile_pool(name="hid", bufs=3))
-        soft_pool = ctx.enter_context(tc.tile_pool(name="soft", bufs=4))
+        soft_pool = ctx.enter_context(tc.tile_pool(name="soft", bufs=6))
         psum_tp = ctx.enter_context(tc.psum_pool(name="psum_tp", bufs=2))
         psum_pre = ctx.enter_context(tc.psum_pool(name="psum_pre", bufs=4))
         psum_att = ctx.enter_context(tc.psum_pool(name="psum_att", bufs=2))
 
-        h_sb = keep.tile([P, NH, TOKENS // P, HD], BF16)
+        h_sb = keep.tile([P, NH, CHUNKS, BLOCKS, HD], BF16)
         w1_sb = keep.tile([P, NH, PASSES, PACK, HD], BF16)
-        hT = keep.tile([P, NH, F_TILES, TOKENS], BF16)
+        hT = keep.tile([P, NH, F_TILES, CHUNKS, BLOCKS, P], BF16)
         w1T = keep.tile([P, NH, F_TILES, PASSES, PACK, P], BF16)
         bias = keep.tile([P, NH, PASSES, PACK], BF16)
         w2_words = keep.tile([P, NH * PASSES, HD], U32, align_bytes=64)
@@ -51,180 +57,217 @@ def tile_multiheadgeneralizedpooling_pa_e_kernel(
         log_mask = keep.tile([P, TOKENS], F32)
         ident_bf = keep.tile([P, P], BF16)
         ident_f32 = keep.tile([P, P], F32)
-        den = keep.tile([P, B * NH * F_TILES], F32)
-        num = keep.tile([P, B * NH * F_TILES], F32)
+        columns = B * NH * F_TILES
+        den = keep.tile([P, columns], F32)
+        num = keep.tile([P, columns], F32)
         pooled = keep.tile([P, P], F32)
+        table_warmer = keep.tile([P, 1], F32)
 
+        def quarter_of(j):
+            head, half = j // 4, (j % 4) // 2
+            if j % 2 == 0:
+                return w1_sb, w1T, head, half
+            return h_sb, hT, head, half
+
+        def load_quarter(j):
+            source, unused, head, half = quarter_of(j)
+            if j % 2 == 0:
+                rows = W1[head].rearrange("(g p t) f -> p g t f", g=PASSES, p=P, t=PACK)
+            else:
+                rows = h_heads[head].flatten_outer_dims().rearrange(
+                    "(n j p) f -> p n j f", n=CHUNKS, j=BLOCKS, p=P
+                )
+            nc.sync.dma_start(out=source[:, head, half], in_=rows[:, half])
+
+        def load_w2_words(head):
+            rows = slice(head * PASSES, (head + 1) * PASSES)
+            words = W2_words.rearrange("g p n t -> g p (n t)").bitcast(I32)
+            nc.sync.dma_start(
+                out=w2_words[:, rows, :].bitcast(I32),
+                in_=words[rows].rearrange("g p n -> p g n"),
+            )
+
+        nc.scalar.dma_start(
+            out=mask_all[:], in_=attention_mask.rearrange("b s -> (b s)").partition_broadcast(P)
+        )
+        nc.scalar.dma_start(
+            out=bias[:], in_=b1.rearrange("i (g p t) -> p i g t", g=PASSES, p=P, t=PACK)
+        )
         make_identity(nc, ident_bf[:])
         make_identity(nc, ident_f32[:])
         nc.vector.memset(w2_scales[:].rearrange("p g n -> p (g n)").bitcast(I32), 0)
         nc.vector.memset(pooled[:], 0.0)
-
-        def load_w1(i, g):
-            rows = W1[i].rearrange("(g p t) f -> p g t f", g=PASSES, p=P, t=PACK)
-            nc.sync.dma_start(out=w1_sb[:, i, g], in_=rows[:, g])
-
-        def load_h(i, n):
-            rows = h_heads[i].flatten_outer_dims().rearrange("(j p) f -> p j f", p=P)
-            blocks = slice(n * BLOCKS, (n + 1) * BLOCKS)
-            nc.sync.dma_start(out=h_sb[:, i, blocks], in_=rows[:, blocks])
-
-        def load_w2_words(i):
-            groups = slice(i * PASSES, (i + 1) * PASSES)
-            words = W2_words.rearrange("g p n t -> g p (n t)").bitcast(I32)
-            nc.sync.dma_start(
-                out=w2_words[:, groups, :].bitcast(I32),
-                in_=words[groups].rearrange("g p n -> p g n"),
-            )
-
-        nc.scalar.dma_start(
-            out=bias[:], in_=b1.rearrange("i (g p t) -> p i g t", g=PASSES, p=P, t=PACK)
-        )
-        nc.scalar.dma_start(
-            out=mask_all[:], in_=attention_mask.rearrange("b s -> (b s)").partition_broadcast(P)
-        )
-        load_w1(0, 0)
-        load_h(0, 0)
-        load_w1(0, 1)
-        load_h(0, 1)
-        for quadrant in range(4):
-            nc.sync.dma_start(
-                out=w2_scales[32 * quadrant : 32 * quadrant + 4, :, :].bitcast(I32),
-                in_=W2_scales.bitcast(I32)[:, 4 * quadrant : 4 * quadrant + 4, :].rearrange(
-                    "g r n -> r g n"
-                ),
-            )
-        load_w2_words(0)
-        for i in range(1, NH):
-            load_w1(i, 0)
-            load_w1(i, 1)
-            load_h(i, 0)
-            load_h(i, 1)
-            load_w2_words(i)
+        for head in range(NH):
+            for j in range(4 * head, 4 * head + 4):
+                load_quarter(j)
+            if head == 0:
+                for quadrant in range(4):
+                    nc.sync.dma_start(
+                        out=w2_scales[32 * quadrant : 32 * quadrant + 4, :, :].bitcast(I32),
+                        in_=W2_scales.bitcast(I32)[
+                            :, 4 * quadrant : 4 * quadrant + 4, :
+                        ].rearrange("g r n -> r g n"),
+                    )
+            load_w2_words(head)
 
         nc.scalar.activation(out=log_mask[:], in_=mask_all[:], func=ACT.Ln)
+        nc.scalar.activation(out=table_warmer[:], in_=log_mask[:, 0:1], func=ACT.Exp)
 
-        def transpose_w1(i, g):
-            tp = psum_tp.tile([P, F_TILES, PACK, P], BF16, tag="tp")
-            for c in range(F_TILES):
-                for t in range(PACK):
-                    nc.tensor.transpose(
-                        tp[:, c, t, :], w1_sb[:, i, g, t, c * P : (c + 1) * P], ident_bf[:]
-                    )
-            nc.scalar.copy(out=w1T[:, i, :, g], in_=tp[:])
-
-        def transpose_h(i, n):
+        def transpose_quarter(j):
+            source, transposed, head, half = quarter_of(j)
             tp = psum_tp.tile([P, F_TILES, BLOCKS, P], BF16, tag="tp")
             for c in range(F_TILES):
-                for j in range(BLOCKS):
+                for x in range(BLOCKS):
                     nc.tensor.transpose(
-                        tp[:, c, j, :], h_sb[:, i, n * BLOCKS + j, c * P : (c + 1) * P], ident_bf[:]
+                        tp[:, c, x, :], source[:, head, half, x, c * P : (c + 1) * P], ident_bf[:]
                     )
-            nc.scalar.copy(
-                out=hT[:, i, :, n * CHUNK : (n + 1) * CHUNK],
-                in_=tp[:].rearrange("p c j t -> p c (j t)"),
+            if j < FIRST_QUARTERS:
+                nc.vector.tensor_copy(out=transposed[:, head, :, half], in_=tp[:])
+            else:
+                nc.scalar.copy(out=transposed[:, head, :, half], in_=tp[:])
+
+        by_t = {}
+        grouped = {}
+        codes = {}
+        scales = {}
+        att = {}
+        score = {}
+        neg_max = {}
+        weight = {}
+
+        def hidden(u, t):
+            head, n, g = u // 4, (u // 2) % 2, u % 2
+            if t == 0:
+                by_t[u] = hid_pool.tile([P, PACK, CHUNK], BF16, name="by_t", tag="by_t")
+            pre = psum_pre.tile([P, CHUNK], F32, tag="pre")
+            for c in range(F_TILES):
+                nc.tensor.matmul(
+                    pre[:],
+                    lhsT=w1T[:, head, c, g, t, :],
+                    rhs=hT[:, head, c, n].rearrange("p j x -> p (j x)"),
+                    start=(c == 0),
+                    stop=(c == F_TILES - 1),
+                )
+            nc.scalar.activation(
+                out=by_t[u][:, t, :],
+                in_=pre[:],
+                func=ACT.Relu,
+                bias=bias[:, head, g, t : t + 1],
+                scale=1.0,
             )
 
-        def hidden_group(i, n, g, att):
-            tokens = slice(n * CHUNK, (n + 1) * CHUNK)
-            by_t = hid_pool.tile([P, PACK, CHUNK], BF16, tag="by_t")
-            for t in range(PACK):
-                pre = psum_pre.tile([P, CHUNK], F32, tag="pre")
-                for c in range(F_TILES):
-                    nc.tensor.matmul(
-                        pre[:],
-                        lhsT=w1T[:, i, c, g, t, :],
-                        rhs=hT[:, i, c, tokens],
-                        start=(c == 0),
-                        stop=(c == F_TILES - 1),
-                    )
-                nc.scalar.activation(
-                    out=by_t[:, t, :],
-                    in_=pre[:],
-                    func=ACT.Relu,
-                    bias=bias[:, i, g, t : t + 1],
-                    scale=1.0,
-                )
-            grouped = hid_pool.tile([P, CHUNK, PACK], BF16, tag="grouped", align_bytes=64)
+        def regroup(u):
+            grouped[u] = hid_pool.tile(
+                [P, CHUNK, PACK], BF16, name="grouped", tag="grouped", align_bytes=64
+            )
             nc.vector.tensor_copy(
-                out=grouped[:].rearrange("p (w r) t -> p w t r", r=4),
-                in_=by_t[:].rearrange("p t (w r) -> p w t r", r=4),
+                out=grouped[u][:].rearrange("p (w r) t -> p w t r", r=4),
+                in_=by_t[u][:].rearrange("p t (w r) -> p w t r", r=4),
             )
-            codes = hid_pool.tile([P, CHUNK], U32, tag="codes", align_bytes=64)
-            scales = hid_pool.tile([P, CHUNK], U8, tag="scales", align_bytes=64)
+
+        def quantise(u):
+            codes[u] = hid_pool.tile([P, CHUNK], U32, name="codes", tag="codes", align_bytes=64)
+            scales[u] = hid_pool.tile([P, CHUNK], U8, name="scales", tag="scales", align_bytes=64)
             nc.vector.quantize_mx(
-                out=codes[:].bitcast(FP8X4),
-                scales=scales[:],
-                in_=grouped[:].rearrange("p w t -> p (w t)"),
+                out=codes[u][:].bitcast(FP8X4),
+                scales=scales[u][:],
+                in_=grouped[u][:].rearrange("p w t -> p (w t)"),
             )
-            group = i * PASSES + g
+
+        def second_matmul(u):
+            g = u % 2
             for m in range(F_TILES):
+                r = (u // 2) * F_TILES + m
+                if g == 0:
+                    att[r] = psum_att.tile([P, CHUNK], F32, name="att", tag="att")
                 features = slice(m * P, (m + 1) * P)
                 nc.tensor.matmul_mx(
-                    out=att[m][:],
-                    lhsT=w2_words[:, group, features].bitcast(FP8X4),
-                    lhsT_scale=w2_scales[:, group, features],
-                    rhs=codes[:].bitcast(FP8X4),
-                    rhs_scale=scales[:],
+                    out=att[r][:],
+                    lhsT=w2_words[:, (u // 4) * PASSES + g, features].bitcast(FP8X4),
+                    lhsT_scale=w2_scales[:, (u // 4) * PASSES + g, features],
+                    rhs=codes[u][:].bitcast(FP8X4),
+                    rhs_scale=scales[u][:],
                     start=(g == 0),
                     stop=(g == PASSES - 1),
                 )
 
-        def pool_chunk(i, n, att):
-            for m in range(F_TILES):
-                score = soft_pool.tile([P, SENTENCES, S], F32, tag="score")
-                nc.vector.tensor_tensor(
-                    out=score[:].rearrange("p b s -> p (b s)"),
-                    in0=att[m][:],
-                    in1=log_mask[:, n * CHUNK : (n + 1) * CHUNK],
-                    op=ALU.add,
-                )
-                neg_max = soft_pool.tile([P, SENTENCES], F32, tag="neg_max")
-                nc.vector.tensor_reduce(
-                    out=neg_max[:], in_=score[:], axis=AXIS.X, op=ALU.max, negate=True
-                )
-                for s in range(SENTENCES):
-                    sentence = n * SENTENCES + s
-                    column = (sentence * NH + i) * F_TILES + m
-                    weight = soft_pool.tile([P, S], F32, tag="weight")
-                    nc.scalar.activation(
-                        out=weight[:],
-                        in_=score[:, s, :],
-                        func=ACT.Exp,
-                        bias=neg_max[:, s : s + 1],
-                        scale=1.0,
-                        accum_out=den[:, column : column + 1],
-                    )
-                    weighted = soft_pool.tile([P, S], F32, tag="weighted")
-                    nc.vector.scalar_tensor_tensor(
-                        out=weighted[:],
-                        in0=weight[:],
-                        scalar=1.0,
-                        in1=hT[:, i, m, sentence * S : (sentence + 1) * S],
-                        op0=ALU.mult,
-                        op1=ALU.mult,
-                        accum_out=num[:, column : column + 1],
-                    )
+        def add_mask(r):
+            n = (r // F_TILES) % CHUNKS
+            score[r] = soft_pool.tile([P, SENTENCES, S], F32, name="score", tag="score")
+            nc.vector.tensor_tensor(
+                out=score[r][:].rearrange("p b s -> p (b s)"),
+                in0=att[r][:],
+                in1=log_mask[:, n * CHUNK : (n + 1) * CHUNK],
+                op=ALU.add,
+            )
 
-        transpose_w1(0, 0)
-        transpose_h(0, 0)
-        transpose_w1(0, 1)
-        transpose_h(0, 1)
-        for i in range(NH):
-            for n in range(CHUNKS):
-                att = [
-                    psum_att.tile([P, CHUNK], F32, name="att%d" % m, tag="att")
-                    for m in range(F_TILES)
-                ]
-                for g in range(PASSES):
-                    hidden_group(i, n, g, att)
-                    if i + 1 < NH and n == 0:
-                        transpose_w1(i + 1, g)
-                    if i + 1 < NH and n == 1:
-                        transpose_h(i + 1, g)
-                pool_chunk(i, n, att)
+        def find_max(r):
+            neg_max[r] = soft_pool.tile([P, SENTENCES], F32, name="neg_max", tag="neg_max")
+            nc.vector.tensor_reduce(
+                out=neg_max[r][:], in_=score[r][:], axis=AXIS.X, op=ALU.max, negate=True
+            )
 
-        columns = B * NH * F_TILES
+        def column_of(r, s):
+            head, n, m = r // (CHUNKS * F_TILES), (r // F_TILES) % CHUNKS, r % F_TILES
+            return ((n * SENTENCES + s) * NH + head) * F_TILES + m
+
+        def exponentials(r):
+            for s in range(SENTENCES):
+                weight[r, s] = soft_pool.tile([P, S], F32, name="weight", tag="weight")
+                nc.scalar.activation(
+                    out=weight[r, s][:],
+                    in_=score[r][:, s, :],
+                    func=ACT.Exp,
+                    bias=neg_max[r][:, s : s + 1],
+                    scale=1.0,
+                    accum_out=den[:, column_of(r, s) : column_of(r, s) + 1],
+                )
+
+        def weighted_sums(r):
+            head, n, m = r // (CHUNKS * F_TILES), (r // F_TILES) % CHUNKS, r % F_TILES
+            per_sentence = S // P
+            for s in range(SENTENCES):
+                weighted = soft_pool.tile([P, S], F32, tag="weighted")
+                nc.vector.scalar_tensor_tensor(
+                    out=weighted[:],
+                    in0=weight[r, s][:],
+                    scalar=1.0,
+                    in1=hT[:, head, m, n, s * per_sentence : (s + 1) * per_sentence, :].rearrange(
+                        "p j x -> p (j x)"
+                    ),
+                    op0=ALU.mult,
+                    op1=ALU.mult,
+                    accum_out=num[:, column_of(r, s) : column_of(r, s) + 1],
+                )
+
+        for j in range(FIRST_QUARTERS):
+            transpose_quarter(j)
+        for k in range(GROUPS + 6):
+            if k < GROUPS:
+                hidden(k, 0)
+                hidden(k, 1)
+            if 0 <= k - 5 < HALVES:
+                exponentials(k - 5)
+            if k < GROUPS:
+                hidden(k, 2)
+                hidden(k, 3)
+            if k + FIRST_QUARTERS < QUARTERS:
+                transpose_quarter(k + FIRST_QUARTERS)
+            if 0 <= k - 2 < GROUPS:
+                second_matmul(k - 2)
+            chunk = (k - 3) // 2
+            soft_stage = add_mask if k % 2 == 1 else find_max
+            if 0 <= k - 1 < GROUPS:
+                regroup(k - 1)
+            if 0 <= chunk < NH * CHUNKS:
+                soft_stage(chunk * F_TILES)
+            if 0 <= k - 1 < GROUPS:
+                quantise(k - 1)
+            if 0 <= chunk < NH * CHUNKS:
+                soft_stage(chunk * F_TILES + 1)
+            if 0 <= k - 6 < HALVES:
+                weighted_sums(k - 6)
+
         inv_den = keep.tile([P, columns], F32)
         nc.vector.reciprocal(out=inv_den[:], in_=den[:])
         nc.vector.tensor_mul(out=pooled[:, 0:columns], in0=num[:], in1=inv_den[:])

@@ -40,10 +40,9 @@ def tile_multiheadgeneralizedpooling_pa_e_kernel(
     with ExitStack() as ctx:
         ctx.enter_context(tc.manual_schedule())
         keep = ctx.enter_context(tc.tile_pool(name="keep", bufs=1))
-        hid_pool = ctx.enter_context(tc.tile_pool(name="hid", bufs=3))
+        hid_pool = ctx.enter_context(tc.tile_pool(name="hid", bufs=4))
         soft_pool = ctx.enter_context(tc.tile_pool(name="soft", bufs=6))
-        psum_tp = ctx.enter_context(tc.psum_pool(name="psum_tp", bufs=2))
-        psum_pre = ctx.enter_context(tc.psum_pool(name="psum_pre", bufs=4))
+        psum_work = ctx.enter_context(tc.psum_pool(name="psum_work", bufs=6))
         psum_att = ctx.enter_context(tc.psum_pool(name="psum_att", bufs=2))
 
         h_sb = keep.tile([P, NH, CHUNKS, BLOCKS, HD], BF16)
@@ -115,7 +114,7 @@ def tile_multiheadgeneralizedpooling_pa_e_kernel(
 
         def transpose_quarter(j):
             source, transposed, head, half = quarter_of(j)
-            tp = psum_tp.tile([P, F_TILES, BLOCKS, P], BF16, tag="tp")
+            tp = psum_work.tile([P, F_TILES, BLOCKS, P], BF16, tag="bank")
             for c in range(F_TILES):
                 for x in range(BLOCKS):
                     nc.tensor.transpose(
@@ -139,7 +138,7 @@ def tile_multiheadgeneralizedpooling_pa_e_kernel(
             head, n, g = u // 4, (u // 2) % 2, u % 2
             if t == 0:
                 by_t[u] = hid_pool.tile([P, PACK, CHUNK], BF16, name="by_t", tag="by_t")
-            pre = psum_pre.tile([P, CHUNK], F32, tag="pre")
+            pre = psum_work.tile([P, CHUNK], F32, tag="bank")
             for c in range(F_TILES):
                 nc.tensor.matmul(
                     pre[:],
@@ -251,27 +250,27 @@ def tile_multiheadgeneralizedpooling_pa_e_kernel(
             if k < GROUPS:
                 hidden(k, 2)
                 hidden(k, 3)
-            if k + FIRST_QUARTERS < QUARTERS:
-                transpose_quarter(k + FIRST_QUARTERS)
             if 0 <= k - 2 < GROUPS:
                 second_matmul(k - 2)
+            if k + FIRST_QUARTERS < QUARTERS:
+                transpose_quarter(k + FIRST_QUARTERS)
             chunk = (k - 3) // 2
             soft_stage = add_mask if k % 2 == 1 else find_max
             if 0 <= k - 1 < GROUPS:
                 regroup(k - 1)
+            if 0 <= k - 6 < HALVES:
+                weighted_sums(k - 6)
             if 0 <= chunk < NH * CHUNKS:
                 soft_stage(chunk * F_TILES)
             if 0 <= k - 1 < GROUPS:
                 quantise(k - 1)
             if 0 <= chunk < NH * CHUNKS:
                 soft_stage(chunk * F_TILES + 1)
-            if 0 <= k - 6 < HALVES:
-                weighted_sums(k - 6)
 
         inv_den = keep.tile([P, columns], F32)
         nc.vector.reciprocal(out=inv_den[:], in_=den[:])
         nc.vector.tensor_mul(out=pooled[:, 0:columns], in0=num[:], in1=inv_den[:])
-        pooledT = psum_tp.tile([P, P], F32, tag="tp")
+        pooledT = psum_work.tile([P, P], F32, tag="bank")
         nc.tensor.transpose(pooledT[:], pooled[:], ident_f32[:])
         result = keep.tile([columns, P], F32)
         nc.vector.tensor_copy(out=result[:], in_=pooledT[0:columns, :])

@@ -28,7 +28,8 @@ BLOCKS = CHUNK // P
 GROUPS = NH * CHUNKS * PASSES
 HALVES = NH * CHUNKS * F_TILES
 QUARTERS = NH * 4
-FIRST_QUARTERS = 3
+FIRST_QUARTERS = 2
+AHEAD = 3
 
 FLOPS = 2 * 2 * NH * TOKENS * HID * HD
 
@@ -52,7 +53,8 @@ def tile_multiheadgeneralizedpooling_pa_e_kernel(
         bias = keep.tile([P, NH, PASSES, PACK], BF16)
         w2_words = keep.tile([P, NH * PASSES, HD], U32, align_bytes=64)
         w2_scales = keep.tile([P, NH * PASSES, HD], U8, align_bytes=64)
-        mask_all = keep.tile([P, TOKENS], BF16)
+        mask_row = keep.tile([P, TOKENS], BF16)
+        ones = keep.tile([P, P], BF16)
         log_mask = keep.tile([P, TOKENS], F32)
         ident_bf = keep.tile([P, P], BF16)
         ident_f32 = keep.tile([P, P], F32)
@@ -60,7 +62,7 @@ def tile_multiheadgeneralizedpooling_pa_e_kernel(
         den = keep.tile([P, columns], F32)
         num = keep.tile([P, columns], F32)
         pooled = keep.tile([P, P], F32)
-        table_warmer = keep.tile([P, 1], F32)
+        table_warmer = keep.tile([P, 2], F32)
 
         def quarter_of(j):
             head, half = j // 4, (j % 4) // 2
@@ -86,19 +88,25 @@ def tile_multiheadgeneralizedpooling_pa_e_kernel(
                 in_=words[rows].rearrange("g p n -> p g n"),
             )
 
-        nc.scalar.dma_start(
-            out=mask_all[:], in_=attention_mask.rearrange("b s -> (b s)").partition_broadcast(P)
-        )
-        nc.scalar.dma_start(
-            out=bias[:], in_=b1.rearrange("i (g p t) -> p i g t", g=PASSES, p=P, t=PACK)
-        )
         make_identity(nc, ident_bf[:])
         make_identity(nc, ident_f32[:])
+        nc.vector.memset(table_warmer[:], 1.0)
+        nc.vector.memset(mask_row[:].bitcast(I32), 0)
+        nc.vector.memset(ones[:], 1.0)
         nc.vector.memset(w2_scales[:].rearrange("p g n -> p (g n)").bitcast(I32), 0)
         nc.vector.memset(pooled[:], 0.0)
         for head in range(NH):
             for j in range(4 * head, 4 * head + 4):
                 load_quarter(j)
+                if j == FIRST_QUARTERS - 1:
+                    nc.sync.dma_start(
+                        out=mask_row[0:1, :],
+                        in_=attention_mask.rearrange("b s -> (b s)").unsqueeze(0),
+                    )
+                    nc.sync.dma_start(
+                        out=bias[:],
+                        in_=b1.rearrange("i (g p t) -> p i g t", g=PASSES, p=P, t=PACK),
+                    )
             if head == 0:
                 for quadrant in range(4):
                     nc.sync.dma_start(
@@ -109,8 +117,17 @@ def tile_multiheadgeneralizedpooling_pa_e_kernel(
                     )
             load_w2_words(head)
 
-        nc.scalar.activation(out=log_mask[:], in_=mask_all[:], func=ACT.Ln)
-        nc.scalar.activation(out=table_warmer[:], in_=log_mask[:, 0:1], func=ACT.Exp)
+        nc.scalar.activation(out=table_warmer[:, 1:2], in_=table_warmer[:, 0:1], func=ACT.Ln)
+
+        def log_of_mask():
+            for n in range(CHUNKS):
+                tokens = slice(n * CHUNK, (n + 1) * CHUNK)
+                spread = psum_work.tile([P, CHUNK], F32, tag="bank")
+                nc.tensor.matmul(
+                    spread[:], lhsT=ones[:], rhs=mask_row[:, tokens], start=True, stop=True
+                )
+                nc.scalar.activation(out=log_mask[:, tokens], in_=spread[:], func=ACT.Ln)
+            nc.scalar.activation(out=table_warmer[:, 1:2], in_=table_warmer[:, 0:1], func=ACT.Exp)
 
         def transpose_quarter(j):
             source, transposed, head, half = quarter_of(j)
@@ -120,7 +137,7 @@ def tile_multiheadgeneralizedpooling_pa_e_kernel(
                     nc.tensor.transpose(
                         tp[:, c, x, :], source[:, head, half, x, c * P : (c + 1) * P], ident_bf[:]
                     )
-            if j < FIRST_QUARTERS:
+            if j < 4:
                 nc.vector.tensor_copy(out=transposed[:, head, :, half], in_=tp[:])
             else:
                 nc.scalar.copy(out=transposed[:, head, :, half], in_=tp[:])
@@ -241,31 +258,38 @@ def tile_multiheadgeneralizedpooling_pa_e_kernel(
 
         for j in range(FIRST_QUARTERS):
             transpose_quarter(j)
-        for k in range(GROUPS + 6):
+        log_of_mask()
+        for k in range(GROUPS + 4):
             if k < GROUPS:
                 hidden(k, 0)
                 hidden(k, 1)
-            if 0 <= k - 5 < HALVES:
-                exponentials(k - 5)
+            if 0 <= k - 4 < HALVES:
+                exponentials(k - 4)
             if k < GROUPS:
                 hidden(k, 2)
                 hidden(k, 3)
             if 0 <= k - 2 < GROUPS:
                 second_matmul(k - 2)
-            if k + FIRST_QUARTERS < QUARTERS:
-                transpose_quarter(k + FIRST_QUARTERS)
+            first_quarter = FIRST_QUARTERS if k == 0 else k + AHEAD
+            for j in range(first_quarter, min(k + AHEAD + 1, QUARTERS)):
+                transpose_quarter(j)
             chunk = (k - 3) // 2
-            soft_stage = add_mask if k % 2 == 1 else find_max
+            has_chunk = 0 <= chunk < NH * CHUNKS
+            scores_complete = has_chunk and k % 2 == 1
             if 0 <= k - 1 < GROUPS:
                 regroup(k - 1)
-            if 0 <= k - 6 < HALVES:
-                weighted_sums(k - 6)
-            if 0 <= chunk < NH * CHUNKS:
-                soft_stage(chunk * F_TILES)
+            if scores_complete:
+                add_mask(chunk * F_TILES)
+            if has_chunk and not scores_complete:
+                find_max(chunk * F_TILES + 1)
             if 0 <= k - 1 < GROUPS:
                 quantise(k - 1)
-            if 0 <= chunk < NH * CHUNKS:
-                soft_stage(chunk * F_TILES + 1)
+            if scores_complete:
+                add_mask(chunk * F_TILES + 1)
+            if scores_complete:
+                find_max(chunk * F_TILES)
+            if 0 <= k - 4 < HALVES:
+                weighted_sums(k - 4)
 
         inv_den = keep.tile([P, columns], F32)
         nc.vector.reciprocal(out=inv_den[:], in_=den[:])

@@ -46,12 +46,26 @@ def tile_multiheadgeneralizedpooling_pa_e_kernel(
         psum_work = ctx.enter_context(tc.psum_pool(name="psum_work", bufs=6))
         psum_att = ctx.enter_context(tc.psum_pool(name="psum_att", bufs=2))
 
-        h_sb = keep.tile([P, NH, CHUNKS, BLOCKS, HD], BF16)
-        w1_sb = keep.tile([P, NH, PASSES, PACK, HD], BF16)
-        hT = keep.tile([P, NH, F_TILES, CHUNKS, BLOCKS, P], BF16)
-        w1T = keep.tile([P, NH, F_TILES, PASSES, PACK, P], BF16)
+        h_sb = [
+            [keep.tile([P, BLOCKS, HD], BF16, name="h_sb_%d_%d" % (i, n)) for n in range(CHUNKS)]
+            for i in range(NH)
+        ]
+        w1_sb = [
+            [keep.tile([P, PACK, HD], BF16, name="w1_sb_%d_%d" % (i, g)) for g in range(PASSES)]
+            for i in range(NH)
+        ]
+        hT = [
+            [keep.tile([P, F_TILES, BLOCKS, P], BF16, name="hT_%d_%d" % (i, n)) for n in range(CHUNKS)]
+            for i in range(NH)
+        ]
+        w1T = [
+            [keep.tile([P, F_TILES, PACK, P], BF16, name="w1T_%d_%d" % (i, g)) for g in range(PASSES)]
+            for i in range(NH)
+        ]
         bias = keep.tile([P, NH, PASSES, PACK], BF16)
-        w2_words = keep.tile([P, NH * PASSES, HD], U32, align_bytes=64)
+        w2_words = [
+            keep.tile([P, PASSES, HD], U32, name="w2_words_%d" % i, align_bytes=64) for i in range(NH)
+        ]
         w2_scales = keep.tile([P, NH * PASSES, HD], U8, align_bytes=64)
         mask_row = keep.tile([P, TOKENS], BF16)
         ones = keep.tile([P, P], BF16)
@@ -78,13 +92,13 @@ def tile_multiheadgeneralizedpooling_pa_e_kernel(
                 rows = h_heads[head].flatten_outer_dims().rearrange(
                     "(n j p) f -> p n j f", n=CHUNKS, j=BLOCKS, p=P
                 )
-            nc.sync.dma_start(out=source[:, head, half], in_=rows[:, half])
+            nc.sync.dma_start(out=source[head][half][:], in_=rows[:, half])
 
         def load_w2_words(head):
             rows = slice(head * PASSES, (head + 1) * PASSES)
             words = W2_words.rearrange("g p n t -> g p (n t)").bitcast(I32)
             nc.sync.dma_start(
-                out=w2_words[:, rows, :].bitcast(I32),
+                out=w2_words[head][:].bitcast(I32),
                 in_=words[rows].rearrange("g p n -> p g n"),
             )
 
@@ -135,12 +149,14 @@ def tile_multiheadgeneralizedpooling_pa_e_kernel(
             for c in range(F_TILES):
                 for x in range(BLOCKS):
                     nc.tensor.transpose(
-                        tp[:, c, x, :], source[:, head, half, x, c * P : (c + 1) * P], ident_bf[:]
+                        tp[:, c, x, :], source[head][half][:, x, c * P : (c + 1) * P], ident_bf[:]
                     )
+            words_in = tp[:].rearrange("p c x q -> p c (x q)").bitcast(F32)
+            words_out = transposed[head][half][:].rearrange("p c x q -> p c (x q)").bitcast(F32)
             if j < 4:
-                nc.vector.tensor_copy(out=transposed[:, head, :, half], in_=tp[:])
+                nc.vector.tensor_copy(out=words_out, in_=words_in)
             else:
-                nc.scalar.copy(out=transposed[:, head, :, half], in_=tp[:])
+                nc.scalar.copy(out=words_out, in_=words_in)
 
         by_t = {}
         grouped = {}
@@ -159,8 +175,8 @@ def tile_multiheadgeneralizedpooling_pa_e_kernel(
             for c in range(F_TILES):
                 nc.tensor.matmul(
                     pre[:],
-                    lhsT=w1T[:, head, c, g, t, :],
-                    rhs=hT[:, head, c, n].rearrange("p j x -> p (j x)"),
+                    lhsT=w1T[head][g][:, c, t, :],
+                    rhs=hT[head][n][:, c].rearrange("p j x -> p (j x)"),
                     start=(c == 0),
                     stop=(c == F_TILES - 1),
                 )
@@ -199,7 +215,7 @@ def tile_multiheadgeneralizedpooling_pa_e_kernel(
                 features = slice(m * P, (m + 1) * P)
                 nc.tensor.matmul_mx(
                     out=att[r][:],
-                    lhsT=w2_words[:, (u // 4) * PASSES + g, features].bitcast(FP8X4),
+                    lhsT=w2_words[u // 4][:, g, features].bitcast(FP8X4),
                     lhsT_scale=w2_scales[:, (u // 4) * PASSES + g, features],
                     rhs=codes[u][:].bitcast(FP8X4),
                     rhs_scale=scales[u][:],
@@ -248,7 +264,7 @@ def tile_multiheadgeneralizedpooling_pa_e_kernel(
                     out=weighted[:],
                     in0=weight[r, s][:],
                     scalar=1.0,
-                    in1=hT[:, head, m, n, s * per_sentence : (s + 1) * per_sentence, :].rearrange(
+                    in1=hT[head][n][:, m, s * per_sentence : (s + 1) * per_sentence, :].rearrange(
                         "p j x -> p (j x)"
                     ),
                     op0=ALU.mult,

@@ -31,6 +31,11 @@ QUARTERS = NH * 4
 FIRST_QUARTERS = 2
 AHEAD = 3
 
+WARM = 0
+EARLY_MASK = False
+INTERLEAVE = True
+V_COPIES = 4
+
 FLOPS = 2 * 2 * NH * TOKENS * HID * HD
 
 
@@ -43,7 +48,8 @@ def tile_multiheadgeneralizedpooling_pa_e_kernel(
         keep = ctx.enter_context(tc.tile_pool(name="keep", bufs=1))
         hid_pool = ctx.enter_context(tc.tile_pool(name="hid", bufs=4))
         soft_pool = ctx.enter_context(tc.tile_pool(name="soft", bufs=6))
-        psum_work = ctx.enter_context(tc.psum_pool(name="psum_work", bufs=6))
+        psum_work = ctx.enter_context(tc.psum_pool(name="psum_work", bufs=4 if INTERLEAVE else 6))
+        psum_tp = ctx.enter_context(tc.psum_pool(name="psum_tp", bufs=2)) if INTERLEAVE else psum_work
         psum_att = ctx.enter_context(tc.psum_pool(name="psum_att", bufs=2))
 
         h_sb = [
@@ -104,15 +110,22 @@ def tile_multiheadgeneralizedpooling_pa_e_kernel(
 
         make_identity(nc, ident_bf[:])
         make_identity(nc, ident_f32[:])
-        nc.vector.memset(table_warmer[:], 1.0)
-        nc.vector.memset(mask_row[:].bitcast(I32), 0)
         nc.vector.memset(ones[:], 1.0)
+        nc.vector.memset(mask_row[:].bitcast(I32), 0)
+        nc.vector.memset(table_warmer[:], 1.0)
+        if EARLY_MASK:
+            nc.scalar.dma_start(
+                out=mask_row[0:1, :], in_=attention_mask.rearrange("b s -> (b s)").unsqueeze(0)
+            )
+            nc.scalar.dma_start(
+                out=bias[:], in_=b1.rearrange("i (g p t) -> p i g t", g=PASSES, p=P, t=PACK)
+            )
         nc.vector.memset(w2_scales[:].rearrange("p g n -> p (g n)").bitcast(I32), 0)
         nc.vector.memset(pooled[:], 0.0)
         for head in range(NH):
             for j in range(4 * head, 4 * head + 4):
                 load_quarter(j)
-                if j == FIRST_QUARTERS - 1:
+                if j == FIRST_QUARTERS - 1 and not EARLY_MASK:
                     nc.sync.dma_start(
                         out=mask_row[0:1, :],
                         in_=attention_mask.rearrange("b s -> (b s)").unsqueeze(0),
@@ -143,17 +156,27 @@ def tile_multiheadgeneralizedpooling_pa_e_kernel(
                 nc.scalar.activation(out=log_mask[:, tokens], in_=spread[:], func=ACT.Ln)
             nc.scalar.activation(out=table_warmer[:, 1:2], in_=table_warmer[:, 0:1], func=ACT.Exp)
 
-        def transpose_quarter(j):
+        def open_quarter(j):
             source, transposed, head, half = quarter_of(j)
-            tp = psum_work.tile([P, F_TILES, BLOCKS, P], BF16, tag="bank")
-            for c in range(F_TILES):
-                for x in range(BLOCKS):
-                    nc.tensor.transpose(
-                        tp[:, c, x, :], source[head][half][:, x, c * P : (c + 1) * P], ident_bf[:]
-                    )
+            tp = psum_tp.tile([P, F_TILES, BLOCKS, P], BF16, name="tp", tag="tp" if INTERLEAVE else "bank")
+            pairs = [
+                (tp[:, c, x, :], source[head][half][:, x, c * P : (c + 1) * P])
+                for c in range(F_TILES)
+                for x in range(BLOCKS)
+            ]
+            return tp, pairs
+
+        def transpose_quarter(j):
+            tp, pairs = open_quarter(j)
+            for target, block in pairs:
+                nc.tensor.transpose(target, block, ident_bf[:])
+            copy_quarter(j, tp)
+
+        def copy_quarter(j, tp):
+            source, transposed, head, half = quarter_of(j)
             words_in = tp[:].rearrange("p c x q -> p c (x q)").bitcast(F32)
             words_out = transposed[head][half][:].rearrange("p c x q -> p c (x q)").bitcast(F32)
-            if j < 4:
+            if j < V_COPIES:
                 nc.vector.tensor_copy(out=words_out, in_=words_in)
             else:
                 nc.scalar.copy(out=words_out, in_=words_in)
@@ -167,7 +190,7 @@ def tile_multiheadgeneralizedpooling_pa_e_kernel(
         neg_max = {}
         weight = {}
 
-        def hidden(u, t):
+        def hidden(u, t, woven=()):
             head, n, g = u // 4, (u // 2) % 2, u % 2
             if t == 0:
                 by_t[u] = hid_pool.tile([P, PACK, CHUNK], BF16, name="by_t", tag="by_t")
@@ -180,6 +203,9 @@ def tile_multiheadgeneralizedpooling_pa_e_kernel(
                     start=(c == 0),
                     stop=(c == F_TILES - 1),
                 )
+                share = len(woven) // F_TILES
+                for target, block in woven[c * share : (c + 1) * share]:
+                    nc.tensor.transpose(target, block, ident_bf[:])
             nc.scalar.activation(
                 out=by_t[u][:, t, :],
                 in_=pre[:],
@@ -272,23 +298,37 @@ def tile_multiheadgeneralizedpooling_pa_e_kernel(
                     accum_out=num[:, column_of(r, s) : column_of(r, s) + 1],
                 )
 
+        if WARM:
+            junk = psum_work.tile([P, CHUNK], F32, tag="bank")
+            for i in range(WARM):
+                nc.tensor.matmul(junk[:, 0:P], lhsT=ones[:], rhs=ones[:], start=True, stop=True)
+        if EARLY_MASK:
+            log_of_mask()
         for j in range(FIRST_QUARTERS):
             transpose_quarter(j)
-        log_of_mask()
+        if not EARLY_MASK:
+            log_of_mask()
         for k in range(GROUPS + 4):
+            first_quarter = FIRST_QUARTERS if k == 0 else k + AHEAD
+            quarters = list(range(first_quarter, min(k + AHEAD + 1, QUARTERS)))
+            opened = [(j, open_quarter(j)) for j in quarters] if INTERLEAVE else []
+            woven = [pair for j, (tp, pairs) in opened for pair in pairs]
+            share = len(woven) // PACK
             if k < GROUPS:
-                hidden(k, 0)
-                hidden(k, 1)
+                hidden(k, 0, woven[0:share])
+                hidden(k, 1, woven[share : 2 * share])
             if 0 <= k - 4 < HALVES:
                 exponentials(k - 4)
             if k < GROUPS:
-                hidden(k, 2)
-                hidden(k, 3)
+                hidden(k, 2, woven[2 * share : 3 * share])
+                hidden(k, 3, woven[3 * share : 4 * share])
             if 0 <= k - 2 < GROUPS:
                 second_matmul(k - 2)
-            first_quarter = FIRST_QUARTERS if k == 0 else k + AHEAD
-            for j in range(first_quarter, min(k + AHEAD + 1, QUARTERS)):
-                transpose_quarter(j)
+            for j, (tp, pairs) in opened:
+                copy_quarter(j, tp)
+            if not INTERLEAVE:
+                for j in quarters:
+                    transpose_quarter(j)
             chunk = (k - 3) // 2
             has_chunk = 0 <= chunk < NH * CHUNKS
             scores_complete = has_chunk and k % 2 == 1

@@ -35,6 +35,11 @@ WARM = 0
 EARLY_MASK = False
 INTERLEAVE = True
 V_COPIES = 4
+PE_EVERY = 3
+
+
+def bias_on_tensor(u):
+    return u % PE_EVERY == 0 and u > 0
 
 FLOPS = 2 * 2 * NH * TOKENS * HID * HD
 
@@ -192,6 +197,9 @@ def tile_multiheadgeneralizedpooling_pa_e_kernel(
 
         def hidden(u, t, woven=()):
             head, n, g = u // 4, (u // 2) % 2, u % 2
+            if bias_on_tensor(u):
+                hidden_block(u, t, woven)
+                return
             if t == 0:
                 by_t[u] = hid_pool.tile([P, PACK, CHUNK], BF16, name="by_t", tag="by_t")
             pre = psum_work.tile([P, CHUNK], F32, tag="bank")
@@ -214,7 +222,41 @@ def tile_multiheadgeneralizedpooling_pa_e_kernel(
                 scale=1.0,
             )
 
+        def hidden_block(u, j, woven):
+            head, n, g = u // 4, (u // 2) % 2, u % 2
+            if j == 0:
+                grouped[u] = hid_pool.tile(
+                    [P, CHUNK, PACK], BF16, name="grouped", tag="grouped", align_bytes=64
+                )
+            pre = psum_work.tile([P, PACK, P], F32, tag="bank")
+            for t in range(PACK):
+                nc.tensor.matmul(
+                    pre[:, t, :],
+                    lhsT=ident_bf[:],
+                    rhs=bias[:, head, g, t : t + 1].to_broadcast([P, P]),
+                    start=True,
+                    stop=False,
+                )
+                for c in range(F_TILES):
+                    nc.tensor.matmul(
+                        pre[:, t, :],
+                        lhsT=w1T[head][g][:, c, t, :],
+                        rhs=hT[head][n][:, c, j, :],
+                        start=False,
+                        stop=(c == F_TILES - 1),
+                    )
+                if t % 2 == 1:
+                    for target, block in woven[t // 2 : t // 2 + 1]:
+                        nc.tensor.transpose(target, block, ident_bf[:])
+            nc.scalar.activation(
+                out=grouped[u][:, j * P : (j + 1) * P, :],
+                in_=pre[:].rearrange("p t x -> p x t"),
+                func=ACT.Relu,
+            )
+
         def regroup(u):
+            if bias_on_tensor(u):
+                return
             grouped[u] = hid_pool.tile(
                 [P, CHUNK, PACK], BF16, name="grouped", tag="grouped", align_bytes=64
             )

@@ -34,12 +34,14 @@ AHEAD = 3
 WARM = 0
 EARLY_MASK = False
 INTERLEAVE = True
-V_COPIES = 4
-PE_EVERY = 3
+V_COPIES = 3
+MX_POS = 2
+EXP_POS = 2
+V_GROUPS = 1
 
 
 def bias_on_tensor(u):
-    return u % PE_EVERY == 0 and u > 0
+    return u >= GROUPS // 2 and u % 2 == 1
 
 FLOPS = 2 * 2 * NH * TOKENS * HID * HD
 
@@ -214,6 +216,16 @@ def tile_multiheadgeneralizedpooling_pa_e_kernel(
                 share = len(woven) // F_TILES
                 for target, block in woven[c * share : (c + 1) * share]:
                     nc.tensor.transpose(target, block, ident_bf[:])
+            if u < V_GROUPS:
+                nc.vector.tensor_scalar(
+                    out=by_t[u][:, t, :],
+                    in0=pre[:],
+                    scalar1=bias[:, head, g, t : t + 1],
+                    scalar2=0.0,
+                    op0=ALU.add,
+                    op1=ALU.max,
+                )
+                return
             nc.scalar.activation(
                 out=by_t[u][:, t, :],
                 in_=pre[:],
@@ -356,18 +368,17 @@ def tile_multiheadgeneralizedpooling_pa_e_kernel(
             opened = [(j, open_quarter(j)) for j in quarters] if INTERLEAVE else []
             woven = [pair for j, (tp, pairs) in opened for pair in pairs]
             share = len(woven) // PACK
-            if k < GROUPS:
-                hidden(k, 0, woven[0:share])
-                hidden(k, 1, woven[share : 2 * share])
-            if 0 <= k - 4 < HALVES:
-                exponentials(k - 4)
-            if k < GROUPS:
-                hidden(k, 2, woven[2 * share : 3 * share])
-                hidden(k, 3, woven[3 * share : 4 * share])
-            if 0 <= k - 2 < GROUPS:
-                second_matmul(k - 2)
-            for j, (tp, pairs) in opened:
-                copy_quarter(j, tp)
+            banks_each = PACK // max(len(opened), 1)
+            for t in range(PACK + 1):
+                if t == MX_POS and 0 <= k - 2 < GROUPS:
+                    second_matmul(k - 2)
+                if t == EXP_POS and 0 <= k - 4 < HALVES:
+                    exponentials(k - 4)
+                if t < PACK and k < GROUPS:
+                    hidden(k, t, woven[t * share : (t + 1) * share])
+                    if opened and (t + 1) % banks_each == 0:
+                        j, (tp, pairs) = opened[t // banks_each]
+                        copy_quarter(j, tp)
             if not INTERLEAVE:
                 for j in quarters:
                     transpose_quarter(j)

@@ -31,10 +31,12 @@ QUARTERS = NH * 4
 FIRST_QUARTERS = 2
 AHEAD = 3
 
-WARM = 0
+WARM = 16
 EARLY_MASK = False
 INTERLEAVE = True
 V_COPIES = 3
+MX_BATCH = True
+NO_TR_BEFORE_MX = True
 MX_POS = 2
 EXP_POS = 2
 V_GROUPS = 1
@@ -197,10 +199,10 @@ def tile_multiheadgeneralizedpooling_pa_e_kernel(
         neg_max = {}
         weight = {}
 
-        def hidden(u, t, woven=()):
+        def hidden(u, t, woven=(), end_plain=False):
             head, n, g = u // 4, (u // 2) % 2, u % 2
             if bias_on_tensor(u):
-                hidden_block(u, t, woven)
+                hidden_block(u, t, woven, end_plain)
                 return
             if t == 0:
                 by_t[u] = hid_pool.tile([P, PACK, CHUNK], BF16, name="by_t", tag="by_t")
@@ -214,7 +216,10 @@ def tile_multiheadgeneralizedpooling_pa_e_kernel(
                     stop=(c == F_TILES - 1),
                 )
                 share = len(woven) // F_TILES
-                for target, block in woven[c * share : (c + 1) * share]:
+                mine = woven[c * share : (c + 1) * share]
+                if end_plain:
+                    mine = woven if c == 0 else ()
+                for target, block in mine:
                     nc.tensor.transpose(target, block, ident_bf[:])
             if u < V_GROUPS:
                 nc.vector.tensor_scalar(
@@ -234,7 +239,7 @@ def tile_multiheadgeneralizedpooling_pa_e_kernel(
                 scale=1.0,
             )
 
-        def hidden_block(u, j, woven):
+        def hidden_block(u, j, woven, end_plain=False):
             head, n, g = u // 4, (u // 2) % 2, u % 2
             if j == 0:
                 grouped[u] = hid_pool.tile(
@@ -257,7 +262,7 @@ def tile_multiheadgeneralizedpooling_pa_e_kernel(
                         start=False,
                         stop=(c == F_TILES - 1),
                     )
-                if t % 2 == 1:
+                if t % 2 == (0 if end_plain else 1):
                     for target, block in woven[t // 2 : t // 2 + 1]:
                         nc.tensor.transpose(target, block, ident_bf[:])
             nc.scalar.activation(
@@ -302,6 +307,23 @@ def tile_multiheadgeneralizedpooling_pa_e_kernel(
                     start=(g == 0),
                     stop=(g == PASSES - 1),
                 )
+
+        def second_matmul_chunk(chunk):
+            for m in range(F_TILES):
+                r = chunk * F_TILES + m
+                att[r] = psum_att.tile([P, CHUNK], F32, name="att", tag="att")
+                features = slice(m * P, (m + 1) * P)
+                for g in range(PASSES):
+                    u = chunk * PASSES + g
+                    nc.tensor.matmul_mx(
+                        out=att[r][:],
+                        lhsT=w2_words[u // 4][:, g, features].bitcast(FP8X4),
+                        lhsT_scale=w2_scales[:, (u // 4) * PASSES + g, features],
+                        rhs=codes[u][:].bitcast(FP8X4),
+                        rhs_scale=scales[u][:],
+                        start=(g == 0),
+                        stop=(g == PASSES - 1),
+                    )
 
         def add_mask(r):
             n = (r // F_TILES) % CHUNKS
@@ -370,12 +392,16 @@ def tile_multiheadgeneralizedpooling_pa_e_kernel(
             share = len(woven) // PACK
             banks_each = PACK // max(len(opened), 1)
             for t in range(PACK + 1):
-                if t == MX_POS and 0 <= k - 2 < GROUPS:
-                    second_matmul(k - 2)
+                mx_here = 0 <= k - 2 < GROUPS and (k % 2 == 1 or not MX_BATCH)
+                if t == MX_POS and mx_here:
+                    if MX_BATCH:
+                        second_matmul_chunk((k - 3) // 2)
+                    else:
+                        second_matmul(k - 2)
                 if t == EXP_POS and 0 <= k - 4 < HALVES:
                     exponentials(k - 4)
                 if t < PACK and k < GROUPS:
-                    hidden(k, t, woven[t * share : (t + 1) * share])
+                    hidden(k, t, woven[t * share : (t + 1) * share], NO_TR_BEFORE_MX and mx_here and t + 1 == MX_POS)
                     if opened and (t + 1) % banks_each == 0:
                         j, (tp, pairs) = opened[t // banks_each]
                         copy_quarter(j, tp)

@@ -31,7 +31,7 @@ QUARTERS = NH * 4
 FIRST_QUARTERS = 2
 AHEAD = 3
 
-WARM = 16
+WARM = 12
 EARLY_MASK = False
 INTERLEAVE = True
 V_COPIES = 3
@@ -42,8 +42,17 @@ EXP_POS = 2
 V_GROUPS = 1
 
 
+LAST_GROUPS = (GROUPS - 2, GROUPS - 1)
+PE_FROM = 6
+PE_EVERY = 3
+
+
+def by_sentence(u):
+    return u in LAST_GROUPS
+
+
 def bias_on_tensor(u):
-    return u >= GROUPS // 2 and u % 2 == 1
+    return by_sentence(u) or (u >= PE_FROM and u % PE_EVERY == 0)
 
 FLOPS = 2 * 2 * NH * TOKENS * HID * HD
 
@@ -241,7 +250,10 @@ def tile_multiheadgeneralizedpooling_pa_e_kernel(
 
         def hidden_block(u, j, woven, end_plain=False):
             head, n, g = u // 4, (u // 2) % 2, u % 2
-            if j == 0:
+            slot = j
+            if by_sentence(u):
+                g, j = slot // 2, (S // P) * (u % 2) + slot % 2
+            if slot == 0:
                 grouped[u] = hid_pool.tile(
                     [P, CHUNK, PACK], BF16, name="grouped", tag="grouped", align_bytes=64
                 )
@@ -266,7 +278,7 @@ def tile_multiheadgeneralizedpooling_pa_e_kernel(
                     for target, block in woven[t // 2 : t // 2 + 1]:
                         nc.tensor.transpose(target, block, ident_bf[:])
             nc.scalar.activation(
-                out=grouped[u][:, j * P : (j + 1) * P, :],
+                out=grouped[u][:, slot * P : (slot + 1) * P, :],
                 in_=pre[:].rearrange("p t x -> p x t"),
                 func=ACT.Relu,
             )
@@ -325,9 +337,33 @@ def tile_multiheadgeneralizedpooling_pa_e_kernel(
                         stop=(g == PASSES - 1),
                     )
 
+        def second_matmul_sentence(u):
+            att[u] = psum_tp.tile([P, F_TILES, S], F32, name="tp", tag="tp")
+            for m in range(F_TILES):
+                features = slice(m * P, (m + 1) * P)
+                for g in range(PASSES):
+                    nc.tensor.matmul_mx(
+                        out=att[u][:, m, :],
+                        lhsT=w2_words[u // 4][:, g, features].bitcast(FP8X4),
+                        lhsT_scale=w2_scales[:, (u // 4) * PASSES + g, features],
+                        rhs=codes[u][:, g * S : (g + 1) * S].bitcast(FP8X4),
+                        rhs_scale=scales[u][:, g * S : (g + 1) * S],
+                        start=(g == 0),
+                        stop=(g == PASSES - 1),
+                    )
+
         def add_mask(r):
             n = (r // F_TILES) % CHUNKS
             score[r] = soft_pool.tile([P, SENTENCES, S], F32, name="score", tag="score")
+            if by_sentence(r):
+                first = n * CHUNK + (r % 2) * S
+                nc.vector.tensor_tensor(
+                    out=score[r][:],
+                    in0=att[r][:],
+                    in1=log_mask[:, first : first + S].unsqueeze(1).to_broadcast([P, F_TILES, S]),
+                    op=ALU.add,
+                )
+                return
             nc.vector.tensor_tensor(
                 out=score[r][:].rearrange("p b s -> p (b s)"),
                 in0=att[r][:],
@@ -343,6 +379,8 @@ def tile_multiheadgeneralizedpooling_pa_e_kernel(
 
         def column_of(r, s):
             head, n, m = r // (CHUNKS * F_TILES), (r // F_TILES) % CHUNKS, r % F_TILES
+            if by_sentence(r):
+                m, s = s, m
             return ((n * SENTENCES + s) * NH + head) * F_TILES + m
 
         def exponentials(r):
@@ -362,11 +400,12 @@ def tile_multiheadgeneralizedpooling_pa_e_kernel(
             per_sentence = S // P
             for s in range(SENTENCES):
                 weighted = soft_pool.tile([P, S], F32, tag="weighted")
+                tile_m, sent = (s, m) if by_sentence(r) else (m, s)
                 nc.vector.scalar_tensor_tensor(
                     out=weighted[:],
                     in0=weight[r, s][:],
                     scalar=1.0,
-                    in1=hT[head][n][:, m, s * per_sentence : (s + 1) * per_sentence, :].rearrange(
+                    in1=hT[head][n][:, tile_m, sent * per_sentence : (sent + 1) * per_sentence, :].rearrange(
                         "p j x -> p (j x)"
                     ),
                     op0=ALU.mult,
@@ -384,7 +423,7 @@ def tile_multiheadgeneralizedpooling_pa_e_kernel(
             transpose_quarter(j)
         if not EARLY_MASK:
             log_of_mask()
-        for k in range(GROUPS + 4):
+        for k in range(GROUPS - 1):
             first_quarter = FIRST_QUARTERS if k == 0 else k + AHEAD
             quarters = list(range(first_quarter, min(k + AHEAD + 1, QUARTERS)))
             opened = [(j, open_quarter(j)) for j in quarters] if INTERLEAVE else []
@@ -425,6 +464,35 @@ def tile_multiheadgeneralizedpooling_pa_e_kernel(
                 find_max(chunk * F_TILES)
             if 0 <= k - 4 < HALVES:
                 weighted_sums(k - 4)
+
+        first, last = LAST_GROUPS
+        quantise(first)
+        hidden(last, 0)
+        hidden(last, 1)
+        second_matmul_chunk(first // 2 - 1)
+        exponentials(first - 3)
+        hidden(last, 2)
+        second_matmul_sentence(first)
+        hidden(last, 3)
+        add_mask(first - 2)
+        add_mask(first - 1)
+        find_max(first - 2)
+        weighted_sums(first - 3)
+        exponentials(first - 2)
+        add_mask(first)
+        find_max(first - 1)
+        exponentials(first - 1)
+        find_max(first)
+        exponentials(first)
+        quantise(last)
+        second_matmul_sentence(last)
+        weighted_sums(first - 2)
+        add_mask(last)
+        weighted_sums(first - 1)
+        find_max(last)
+        exponentials(last)
+        weighted_sums(first)
+        weighted_sums(last)
 
         inv_den = keep.tile([P, columns], F32)
         nc.vector.reciprocal(out=inv_den[:], in_=den[:])

@@ -44,6 +44,8 @@ V_GROUPS = 1
 
 LAST_GROUPS = (GROUPS - 2, GROUPS - 1)
 PE_FROM = 6
+FIRST_PIECES = (2, 4)
+FIRST_ORDER = (1, 0)
 PE_EVERY = 3
 
 
@@ -83,7 +85,7 @@ def tile_multiheadgeneralizedpooling_pa_e_kernel(
             for i in range(NH)
         ]
         w1T = [
-            [keep.tile([P, F_TILES, PACK, P], BF16, name="w1T_%d_%d" % (i, g)) for g in range(PASSES)]
+            [keep.tile([P, PACK, F_TILES, P], BF16, name="w1T_%d_%d" % (i, g)) for g in range(PASSES)]
             for i in range(NH)
         ]
         bias = keep.tile([P, NH, PASSES, PACK], BF16)
@@ -116,7 +118,11 @@ def tile_multiheadgeneralizedpooling_pa_e_kernel(
                 rows = h_heads[head].flatten_outer_dims().rearrange(
                     "(n j p) f -> p n j f", n=CHUNKS, j=BLOCKS, p=P
                 )
-            nc.sync.dma_start(out=source[head][half][:], in_=rows[:, half])
+            pieces = FIRST_PIECES[j] if j < FIRST_QUARTERS else 1
+            width = BLOCKS // pieces
+            for i in range(pieces):
+                part = slice(i * width, (i + 1) * width)
+                nc.sync.dma_start(out=source[head][half][:, part, :], in_=rows[:, half][:, part, :])
 
         def load_w2_words(head):
             rows = slice(head * PASSES, (head + 1) * PASSES)
@@ -141,9 +147,9 @@ def tile_multiheadgeneralizedpooling_pa_e_kernel(
         nc.vector.memset(w2_scales[:].rearrange("p g n -> p (g n)").bitcast(I32), 0)
         nc.vector.memset(pooled[:], 0.0)
         for head in range(NH):
-            for j in range(4 * head, 4 * head + 4):
+            for j in (list(FIRST_ORDER) + [2, 3] if head == 0 else range(4 * head, 4 * head + 4)):
                 load_quarter(j)
-                if j == FIRST_QUARTERS - 1 and not EARLY_MASK:
+                if j == FIRST_ORDER[-1] and not EARLY_MASK:
                     nc.sync.dma_start(
                         out=mask_row[0:1, :],
                         in_=attention_mask.rearrange("b s -> (b s)").unsqueeze(0),
@@ -176,12 +182,13 @@ def tile_multiheadgeneralizedpooling_pa_e_kernel(
 
         def open_quarter(j):
             source, transposed, head, half = quarter_of(j)
-            tp = psum_tp.tile([P, F_TILES, BLOCKS, P], BF16, name="tp", tag="tp" if INTERLEAVE else "bank")
-            pairs = [
-                (tp[:, c, x, :], source[head][half][:, x, c * P : (c + 1) * P])
-                for c in range(F_TILES)
-                for x in range(BLOCKS)
-            ]
+            if j % 2 == 0:
+                tp = psum_tp.tile([P, PACK, F_TILES, P], BF16, name="tp", tag="tp")
+                slots = [(x, c, tp[:, x, c, :]) for x in range(PACK) for c in range(F_TILES)]
+            else:
+                tp = psum_tp.tile([P, F_TILES, BLOCKS, P], BF16, name="tp", tag="tp")
+                slots = [(x, c, tp[:, c, x, :]) for x in range(BLOCKS) for c in range(F_TILES)]
+            pairs = [(slot, source[head][half][:, x, c * P : (c + 1) * P]) for x, c, slot in slots]
             return tp, pairs
 
         def transpose_quarter(j):
@@ -219,7 +226,7 @@ def tile_multiheadgeneralizedpooling_pa_e_kernel(
             for c in range(F_TILES):
                 nc.tensor.matmul(
                     pre[:],
-                    lhsT=w1T[head][g][:, c, t, :],
+                    lhsT=w1T[head][g][:, t, c, :],
                     rhs=hT[head][n][:, c].rearrange("p j x -> p (j x)"),
                     start=(c == 0),
                     stop=(c == F_TILES - 1),
@@ -269,7 +276,7 @@ def tile_multiheadgeneralizedpooling_pa_e_kernel(
                 for c in range(F_TILES):
                     nc.tensor.matmul(
                         pre[:, t, :],
-                        lhsT=w1T[head][g][:, c, t, :],
+                        lhsT=w1T[head][g][:, t, c, :],
                         rhs=hT[head][n][:, c, j, :],
                         start=False,
                         stop=(c == F_TILES - 1),
@@ -419,8 +426,17 @@ def tile_multiheadgeneralizedpooling_pa_e_kernel(
                 nc.tensor.matmul(junk[:, 0:P], lhsT=ones[:], rhs=ones[:], start=True, stop=True)
         if EARLY_MASK:
             log_of_mask()
-        for j in range(FIRST_QUARTERS):
-            transpose_quarter(j)
+        transpose_quarter(1)
+        tp, pairs = open_quarter(0)
+        for i in range(FIRST_PIECES[0]):
+            width = PACK // FIRST_PIECES[0]
+            for target, block in pairs[i * width * F_TILES : (i + 1) * width * F_TILES]:
+                nc.tensor.transpose(target, block, ident_bf[:])
+            part = slice(i * width, (i + 1) * width)
+            nc.scalar.copy(
+                out=w1T[0][0][:, part].rearrange("p x c q -> p (x c q)").bitcast(F32),
+                in_=tp[:, part].rearrange("p x c q -> p (x c q)").bitcast(F32),
+            )
         if not EARLY_MASK:
             log_of_mask()
         for k in range(GROUPS - 1):

@@ -297,8 +297,8 @@ def tile_multiheadgeneralizedpooling_pa_e_kernel(
                 [P, CHUNK, PACK], BF16, name="grouped", tag="grouped", align_bytes=64
             )
             nc.vector.tensor_copy(
-                out=grouped[u][:].rearrange("p (w r) t -> p w t r", r=4),
-                in_=by_t[u][:].rearrange("p t (w r) -> p w t r", r=4),
+                out=grouped[u][:].rearrange("p (w r) t -> p w t r", r=8),
+                in_=by_t[u][:].rearrange("p t (w r) -> p w t r", r=8),
             )
 
         def quantise(u):

@@ -42,7 +42,9 @@ EXP_POS = 2
 V_GROUPS = 1
 
 
-LAST_GROUPS = (GROUPS - 2, GROUPS - 1)
+LAST = GROUPS - 1
+FIRST_SCALED = HALVES - 3
+LAST_GROUPS = (GROUPS - 2, LAST)
 PE_FROM = 6
 FIRST_PIECES = (2, 4)
 FIRST_ORDER = (1, 0)
@@ -101,6 +103,7 @@ def tile_multiheadgeneralizedpooling_pa_e_kernel(
         columns = B * NH * F_TILES
         den = keep.tile([P, columns], F32)
         num = keep.tile([P, columns], F32)
+        inv_den = keep.tile([P, columns], F32)
         pooled = keep.tile([P, P], F32)
         table_warmer = keep.tile([P, 2], F32)
 
@@ -146,6 +149,8 @@ def tile_multiheadgeneralizedpooling_pa_e_kernel(
             )
         nc.vector.memset(w2_scales[:].rearrange("p g n -> p (g n)").bitcast(I32), 0)
         nc.vector.memset(pooled[:], 0.0)
+        nc.vector.memset(den[:], 1.0)
+        nc.vector.memset(num[:], 0.0)
         for head in range(NH):
             for j in (list(FIRST_ORDER) + [2, 3] if head == 0 else range(4 * head, 4 * head + 4)):
                 load_quarter(j)
@@ -213,6 +218,7 @@ def tile_multiheadgeneralizedpooling_pa_e_kernel(
         att = {}
         score = {}
         neg_max = {}
+        product = {}
         weight = {}
 
         def hidden(u, t, woven=(), end_plain=False):
@@ -259,7 +265,8 @@ def tile_multiheadgeneralizedpooling_pa_e_kernel(
             head, n, g = u // 4, (u // 2) % 2, u % 2
             slot = j
             if by_sentence(u):
-                g, j = slot // 2, (S // P) * (u % 2) + slot % 2
+                x, g = (slot // 2, slot % 2) if u == LAST else (slot % 2, slot // 2)
+                j = (S // P) * (u % 2) + x
             if slot == 0:
                 grouped[u] = hid_pool.tile(
                     [P, CHUNK, PACK], BF16, name="grouped", tag="grouped", align_bytes=64
@@ -359,6 +366,82 @@ def tile_multiheadgeneralizedpooling_pa_e_kernel(
                         stop=(g == PASSES - 1),
                     )
 
+        def quantise_block(x):
+            u = LAST
+            width = PASSES * P
+            codes[u, x] = hid_pool.tile([P, width], U32, name="codes", tag="codes", align_bytes=64)
+            scales[u, x] = hid_pool.tile([P, width], U8, name="scales", tag="scales", align_bytes=64)
+            nc.vector.quantize_mx(
+                out=codes[u, x][:].bitcast(FP8X4),
+                scales=scales[u, x][:],
+                in_=grouped[u][:, x * width : (x + 1) * width, :].rearrange("p w t -> p (w t)"),
+            )
+
+        def second_matmul_block(x):
+            u = LAST
+            pool, tag = ((psum_tp, "tp"), (psum_att, "att"))[x]
+            att[u, x] = pool.tile([P, F_TILES, P], F32, name="att_block", tag=tag)
+            for m in range(F_TILES):
+                features = slice(m * P, (m + 1) * P)
+                for g in range(PASSES):
+                    nc.tensor.matmul_mx(
+                        out=att[u, x][:, m, :],
+                        lhsT=w2_words[u // 4][:, g, features].bitcast(FP8X4),
+                        lhsT_scale=w2_scales[:, (u // 4) * PASSES + g, features],
+                        rhs=codes[u, x][:, g * P : (g + 1) * P].bitcast(FP8X4),
+                        rhs_scale=scales[u, x][:, g * P : (g + 1) * P],
+                        start=(g == 0),
+                        stop=(g == PASSES - 1),
+                    )
+
+        def add_mask_block(x):
+            if x == 0:
+                score[LAST] = soft_pool.tile([P, F_TILES, S + 1], F32, name="score", tag="score_last")
+            first = TOKENS - S + x * P
+            nc.vector.tensor_tensor(
+                out=score[LAST][:, :, x * P : (x + 1) * P],
+                in0=att[LAST, x][:],
+                in1=log_mask[:, first : first + P].unsqueeze(1).to_broadcast([P, F_TILES, P]),
+                op=ALU.add,
+            )
+
+        def find_max_block(x):
+            if x == 0:
+                nc.vector.tensor_reduce(
+                    out=score[LAST][:, :, S], in_=score[LAST][:, :, 0:P], axis=AXIS.X, op=ALU.max
+                )
+                return
+            neg_max[LAST] = soft_pool.tile([P, SENTENCES], F32, name="neg_max", tag="neg_max")
+            nc.vector.tensor_reduce(
+                out=neg_max[LAST][:], in_=score[LAST][:, :, P : S + 1], axis=AXIS.X, op=ALU.max, negate=True
+            )
+
+        def products(r):
+            head, n, m = r // (CHUNKS * F_TILES), (r // F_TILES) % CHUNKS, r % F_TILES
+            per_sentence = S // P
+            for s in range(SENTENCES):
+                tile_m, sent = (s, m) if by_sentence(r) else (m, s)
+                product[r, s] = soft_pool.tile([P, S], F32, name="product", tag="product")
+                nc.gpsimd.tensor_tensor(
+                    out=product[r, s][:],
+                    in0=weight[r, s][:],
+                    in1=hT[head][n][:, tile_m, sent * per_sentence : (sent + 1) * per_sentence, :].rearrange(
+                        "p j x -> p (j x)"
+                    ),
+                    op=ALU.mult,
+                )
+
+        def sums(r):
+            for s in range(SENTENCES):
+                column = slice(column_of(r, s), column_of(r, s) + 1)
+                nc.scalar.activation(
+                    out=weight[r, s][:],
+                    in_=product[r, s][:],
+                    func=ACT.Copy,
+                    scale=inv_den[:, column] if r >= FIRST_SCALED else 1.0,
+                    accum_out=(pooled if r >= FIRST_SCALED else num)[:, column],
+                )
+
         def add_mask(r):
             n = (r // F_TILES) % CHUNKS
             score[r] = soft_pool.tile([P, SENTENCES, S], F32, name="score", tag="score")
@@ -395,29 +478,41 @@ def tile_multiheadgeneralizedpooling_pa_e_kernel(
                 weight[r, s] = soft_pool.tile([P, S], F32, name="weight", tag="weight")
                 nc.scalar.activation(
                     out=weight[r, s][:],
-                    in_=score[r][:, s, :],
+                    in_=score[r][:, s, 0:S],
                     func=ACT.Exp,
                     bias=neg_max[r][:, s : s + 1],
                     scale=1.0,
                     accum_out=den[:, column_of(r, s) : column_of(r, s) + 1],
                 )
 
-        def weighted_sums(r):
+        def invert_all():
+            nc.vector.reciprocal(out=inv_den[:], in_=den[:])
+
+        def divide_all():
+            nc.vector.tensor_tensor(out=pooled[:, 0:columns], in0=num[:], in1=inv_den[:], op=ALU.mult)
+
+        def invert(r, which=tuple(range(SENTENCES))):
+            cols = [column_of(r, s) for s in which]
+            part = slice(cols[0], cols[-1] + 1, max(cols[-1] - cols[0], 1))
+            nc.vector.reciprocal(out=inv_den[:, part], in_=den[:, part])
+
+        def weighted_sums(r, which=tuple(range(SENTENCES))):
             head, n, m = r // (CHUNKS * F_TILES), (r // F_TILES) % CHUNKS, r % F_TILES
             per_sentence = S // P
-            for s in range(SENTENCES):
+            for s in which:
                 weighted = soft_pool.tile([P, S], F32, tag="weighted")
                 tile_m, sent = (s, m) if by_sentence(r) else (m, s)
+                column = slice(column_of(r, s), column_of(r, s) + 1)
                 nc.vector.scalar_tensor_tensor(
                     out=weighted[:],
                     in0=weight[r, s][:],
-                    scalar=1.0,
+                    scalar=inv_den[:, column] if r >= FIRST_SCALED else 1.0,
                     in1=hT[head][n][:, tile_m, sent * per_sentence : (sent + 1) * per_sentence, :].rearrange(
                         "p j x -> p (j x)"
                     ),
                     op0=ALU.mult,
                     op1=ALU.mult,
-                    accum_out=num[:, column_of(r, s) : column_of(r, s) + 1],
+                    accum_out=(pooled if r >= FIRST_SCALED else num)[:, column],
                 )
 
         if WARM:
@@ -483,36 +578,45 @@ def tile_multiheadgeneralizedpooling_pa_e_kernel(
 
         first, last = LAST_GROUPS
         quantise(first)
+        exponentials(first - 3)
         hidden(last, 0)
         hidden(last, 1)
         second_matmul_chunk(first // 2 - 1)
-        exponentials(first - 3)
+        weighted_sums(first - 3)
         hidden(last, 2)
-        second_matmul_sentence(first)
-        hidden(last, 3)
         add_mask(first - 2)
+        hidden(last, 3)
+        quantise_block(0)
+        second_matmul_sentence(first)
+        second_matmul_block(0)
         add_mask(first - 1)
         find_max(first - 2)
-        weighted_sums(first - 3)
-        exponentials(first - 2)
-        add_mask(first)
         find_max(first - 1)
+        quantise_block(1)
+        second_matmul_block(1)
+        exponentials(first - 2)
         exponentials(first - 1)
+        products(first - 2)
+        add_mask(first)
+        add_mask_block(0)
+        sums(first - 2)
         find_max(first)
         exponentials(first)
-        quantise(last)
-        second_matmul_sentence(last)
-        weighted_sums(first - 2)
-        add_mask(last)
-        weighted_sums(first - 1)
-        find_max(last)
+        find_max_block(0)
+        products(first - 1)
+        add_mask_block(1)
+        invert_all()
+        find_max_block(1)
         exponentials(last)
-        weighted_sums(first)
+        divide_all()
+        sums(first - 1)
+        invert(first)
+        weighted_sums(first, (0,))
+        invert(last, (0,))
+        weighted_sums(first, (1,))
+        invert(last, (1,))
         weighted_sums(last)
 
-        inv_den = keep.tile([P, columns], F32)
-        nc.vector.reciprocal(out=inv_den[:], in_=den[:])
-        nc.vector.tensor_mul(out=pooled[:, 0:columns], in0=num[:], in1=inv_den[:])
         pooledT = psum_work.tile([P, P], F32, tag="bank")
         nc.tensor.transpose(pooledT[:], pooled[:], ident_f32[:])
         result = keep.tile([columns, P], F32)

@@ -32,7 +32,6 @@ FIRST_QUARTERS = 2
 AHEAD = 3
 
 WARM = 12
-EARLY_MASK = False
 INTERLEAVE = True
 V_COPIES = 3
 MX_BATCH = True
@@ -46,7 +45,7 @@ LAST = GROUPS - 1
 FIRST_SCALED = HALVES - 3
 LAST_GROUPS = (GROUPS - 2, LAST)
 PE_FROM = 6
-FIRST_PIECES = (2, 4)
+FIRST_PIECES = (2, 2)
 FIRST_ORDER = (1, 0)
 PE_EVERY = 3
 
@@ -140,13 +139,6 @@ def tile_multiheadgeneralizedpooling_pa_e_kernel(
         nc.vector.memset(ones[:], 1.0)
         nc.vector.memset(mask_row[:].bitcast(I32), 0)
         nc.vector.memset(table_warmer[:], 1.0)
-        if EARLY_MASK:
-            nc.scalar.dma_start(
-                out=mask_row[0:1, :], in_=attention_mask.rearrange("b s -> (b s)").unsqueeze(0)
-            )
-            nc.scalar.dma_start(
-                out=bias[:], in_=b1.rearrange("i (g p t) -> p i g t", g=PASSES, p=P, t=PACK)
-            )
         nc.vector.memset(w2_scales[:].rearrange("p g n -> p (g n)").bitcast(I32), 0)
         nc.vector.memset(pooled[:], 0.0)
         nc.vector.memset(den[:], 1.0)
@@ -154,7 +146,7 @@ def tile_multiheadgeneralizedpooling_pa_e_kernel(
         for head in range(NH):
             for j in (list(FIRST_ORDER) + [2, 3] if head == 0 else range(4 * head, 4 * head + 4)):
                 load_quarter(j)
-                if j == FIRST_ORDER[-1] and not EARLY_MASK:
+                if j == FIRST_ORDER[-1]:
                     nc.sync.dma_start(
                         out=mask_row[0:1, :],
                         in_=attention_mask.rearrange("b s -> (b s)").unsqueeze(0),
@@ -519,21 +511,30 @@ def tile_multiheadgeneralizedpooling_pa_e_kernel(
             junk = psum_work.tile([P, CHUNK], F32, tag="bank")
             for i in range(WARM):
                 nc.tensor.matmul(junk[:, 0:P], lhsT=ones[:], rhs=ones[:], start=True, stop=True)
-        if EARLY_MASK:
-            log_of_mask()
-        transpose_quarter(1)
-        tp, pairs = open_quarter(0)
-        for i in range(FIRST_PIECES[0]):
-            width = PACK // FIRST_PIECES[0]
-            for target, block in pairs[i * width * F_TILES : (i + 1) * width * F_TILES]:
-                nc.tensor.transpose(target, block, ident_bf[:])
-            part = slice(i * width, (i + 1) * width)
-            nc.scalar.copy(
-                out=w1T[0][0][:, part].rearrange("p x c q -> p (x c q)").bitcast(F32),
-                in_=tp[:, part].rearrange("p x c q -> p (x c q)").bitcast(F32),
-            )
-        if not EARLY_MASK:
-            log_of_mask()
+        def first_piece(j, part, pool, tag, copy):
+            source, transposed, head, half = quarter_of(j)
+            width = part.stop - part.start
+            if j % 2 == 0:
+                tp = pool.tile([P, width, F_TILES, P], BF16, name="first", tag=tag)
+                target = transposed[head][half][:, part].rearrange("p x c q -> p (x c q)")
+                words_in = tp[:].rearrange("p x c q -> p (x c q)").bitcast(F32)
+                slots = [(x, c, tp[:, x, c, :]) for x in range(width) for c in range(F_TILES)]
+                words_out = target.bitcast(F32)
+            else:
+                tp = pool.tile([P, F_TILES, width, P], BF16, name="first", tag=tag)
+                slots = [(x, c, tp[:, c, x, :]) for x in range(width) for c in range(F_TILES)]
+                words_in = tp[:].rearrange("p c x q -> p c (x q)").bitcast(F32)
+                words_out = transposed[head][half][:, :, part].rearrange("p c x q -> p c (x q)").bitcast(F32)
+            for x, c, slot in slots:
+                block = source[head][half][:, part.start + x, c * P : (c + 1) * P]
+                nc.tensor.transpose(slot, block, ident_bf[:])
+            copy(out=words_out, in_=words_in)
+
+        first_piece(1, slice(0, 2), psum_att, "att", nc.vector.tensor_copy)
+        first_piece(1, slice(2, 4), psum_att, "att", nc.vector.tensor_copy)
+        first_piece(0, slice(0, 2), psum_tp, "tp", nc.scalar.copy)
+        first_piece(0, slice(2, 4), psum_tp, "tp", nc.scalar.copy)
+        log_of_mask()
         for k in range(GROUPS - 1):
             first_quarter = FIRST_QUARTERS if k == 0 else k + AHEAD
             quarters = list(range(first_quarter, min(k + AHEAD + 1, QUARTERS)))

@@ -33,6 +33,7 @@ AHEAD = 3
 
 WARM = 12
 INTERLEAVE = True
+V_LATE = (9, 12, 15)
 V_COPIES = 3
 MX_BATCH = True
 NO_TR_BEFORE_MX = True
@@ -198,7 +199,7 @@ def tile_multiheadgeneralizedpooling_pa_e_kernel(
             source, transposed, head, half = quarter_of(j)
             words_in = tp[:].rearrange("p c x q -> p c (x q)").bitcast(F32)
             words_out = transposed[head][half][:].rearrange("p c x q -> p c (x q)").bitcast(F32)
-            if j < V_COPIES:
+            if j < V_COPIES or j in V_LATE:
                 nc.vector.tensor_copy(out=words_out, in_=words_in)
             else:
                 nc.scalar.copy(out=words_out, in_=words_in)
@@ -264,21 +265,21 @@ def tile_multiheadgeneralizedpooling_pa_e_kernel(
                     [P, CHUNK, PACK], BF16, name="grouped", tag="grouped", align_bytes=64
                 )
             pre = psum_work.tile([P, PACK, P], F32, tag="bank")
+            nc.tensor.matmul(
+                pre[:],
+                lhsT=ident_bf[:],
+                rhs=bias[:, head, g, :].unsqueeze(2).to_broadcast([P, PACK, P]),
+                start=True,
+                stop=False,
+            )
             for t in range(PACK):
-                nc.tensor.matmul(
-                    pre[:, t, :],
-                    lhsT=ident_bf[:],
-                    rhs=bias[:, head, g, t : t + 1].to_broadcast([P, P]),
-                    start=True,
-                    stop=False,
-                )
                 for c in range(F_TILES):
                     nc.tensor.matmul(
                         pre[:, t, :],
                         lhsT=w1T[head][g][:, t, c, :],
                         rhs=hT[head][n][:, c, j, :],
                         start=False,
-                        stop=(c == F_TILES - 1),
+                        stop=(t == PACK - 1 and c == F_TILES - 1),
                     )
                 if t % 2 == (0 if end_plain else 1):
                     for target, block in woven[t // 2 : t // 2 + 1]:
@@ -535,6 +536,7 @@ def tile_multiheadgeneralizedpooling_pa_e_kernel(
         first_piece(0, slice(0, 2), psum_tp, "tp", nc.scalar.copy)
         first_piece(0, slice(2, 4), psum_tp, "tp", nc.scalar.copy)
         log_of_mask()
+        late = []
         for k in range(GROUPS - 1):
             first_quarter = FIRST_QUARTERS if k == 0 else k + AHEAD
             quarters = list(range(first_quarter, min(k + AHEAD + 1, QUARTERS)))
@@ -555,7 +557,10 @@ def tile_multiheadgeneralizedpooling_pa_e_kernel(
                     hidden(k, t, woven[t * share : (t + 1) * share], NO_TR_BEFORE_MX and mx_here and t + 1 == MX_POS)
                     if opened and (t + 1) % banks_each == 0:
                         j, (tp, pairs) = opened[t // banks_each]
-                        copy_quarter(j, tp)
+                        if j in V_LATE:
+                            late.append((j, tp))
+                        else:
+                            copy_quarter(j, tp)
             if not INTERLEAVE:
                 for j in quarters:
                     transpose_quarter(j)
@@ -564,6 +569,8 @@ def tile_multiheadgeneralizedpooling_pa_e_kernel(
             scores_complete = has_chunk and k % 2 == 1
             if 0 <= k - 1 < GROUPS:
                 regroup(k - 1)
+            if late and late[0][0] == k - 1 + AHEAD:
+                copy_quarter(*late.pop())
             if scores_complete:
                 add_mask(chunk * F_TILES)
             if has_chunk and not scores_complete:

@@ -31,7 +31,7 @@ QUARTERS = NH * 4
 FIRST_QUARTERS = 2
 AHEAD = 3
 
-WARM = 12
+WARM = 6
 INTERLEAVE = True
 V_LATE = (9, 12, 15)
 V_COPIES = 3
@@ -43,7 +43,7 @@ V_GROUPS = 1
 
 
 LAST = GROUPS - 1
-FIRST_SCALED = HALVES - 3
+FIRST_SCALED = HALVES - 4
 LAST_GROUPS = (GROUPS - 2, LAST)
 PE_FROM = 6
 FIRST_PIECES = (2, 2)
@@ -142,8 +142,6 @@ def tile_multiheadgeneralizedpooling_pa_e_kernel(
         nc.vector.memset(table_warmer[:], 1.0)
         nc.vector.memset(w2_scales[:].rearrange("p g n -> p (g n)").bitcast(I32), 0)
         nc.vector.memset(pooled[:], 0.0)
-        nc.vector.memset(den[:], 1.0)
-        nc.vector.memset(num[:], 0.0)
         for head in range(NH):
             for j in (list(FIRST_ORDER) + [2, 3] if head == 0 else range(4 * head, 4 * head + 4)):
                 load_quarter(j)
@@ -478,11 +476,25 @@ def tile_multiheadgeneralizedpooling_pa_e_kernel(
                     accum_out=den[:, column_of(r, s) : column_of(r, s) + 1],
                 )
 
-        def invert_all():
-            nc.vector.reciprocal(out=inv_den[:], in_=den[:])
+        def by_row(tile):
+            return tile[:, 0:columns].rearrange("p (b c) -> p b c", b=B)
 
-        def divide_all():
-            nc.vector.tensor_tensor(out=pooled[:, 0:columns], in0=num[:], in1=inv_den[:], op=ALU.mult)
+        whole_heads = slice(0, (NH - 1) * F_TILES)
+
+        def invert_heads():
+            nc.vector.reciprocal(out=by_row(inv_den)[:, :, whole_heads], in_=by_row(den)[:, :, whole_heads])
+
+        def divide_heads():
+            nc.vector.tensor_tensor(
+                out=by_row(pooled)[:, :, whole_heads],
+                in0=by_row(num)[:, :, whole_heads],
+                in1=by_row(inv_den)[:, :, whole_heads],
+                op=ALU.mult,
+            )
+
+        def invert_chunk():
+            part = (slice(None), slice(0, SENTENCES), slice((NH - 1) * F_TILES, NH * F_TILES))
+            nc.vector.reciprocal(out=by_row(inv_den)[part], in_=by_row(den)[part])
 
         def invert(r, which=tuple(range(SENTENCES))):
             cols = [column_of(r, s) for s in which]
@@ -512,7 +524,7 @@ def tile_multiheadgeneralizedpooling_pa_e_kernel(
             junk = psum_work.tile([P, CHUNK], F32, tag="bank")
             for i in range(WARM):
                 nc.tensor.matmul(junk[:, 0:P], lhsT=ones[:], rhs=ones[:], start=True, stop=True)
-        def first_piece(j, part, pool, tag, copy):
+        def first_piece(j, part, pool, tag, copy, plain=False):
             source, transposed, head, half = quarter_of(j)
             width = part.stop - part.start
             if j % 2 == 0:
@@ -528,11 +540,14 @@ def tile_multiheadgeneralizedpooling_pa_e_kernel(
                 words_out = transposed[head][half][:, :, part].rearrange("p c x q -> p c (x q)").bitcast(F32)
             for x, c, slot in slots:
                 block = source[head][half][:, part.start + x, c * P : (c + 1) * P]
-                nc.tensor.transpose(slot, block, ident_bf[:])
+                if plain:
+                    nc.tensor.matmul(slot, lhsT=block, rhs=ident_bf[:], start=True, stop=True)
+                else:
+                    nc.tensor.transpose(slot, block, ident_bf[:])
             copy(out=words_out, in_=words_in)
 
-        first_piece(1, slice(0, 2), psum_att, "att", nc.vector.tensor_copy)
-        first_piece(1, slice(2, 4), psum_att, "att", nc.vector.tensor_copy)
+        first_piece(1, slice(0, 2), psum_att, "att", nc.vector.tensor_copy, True)
+        first_piece(1, slice(2, 4), psum_att, "att", nc.vector.tensor_copy, True)
         first_piece(0, slice(0, 2), psum_tp, "tp", nc.scalar.copy)
         first_piece(0, slice(2, 4), psum_tp, "tp", nc.scalar.copy)
         log_of_mask()
@@ -591,10 +606,12 @@ def tile_multiheadgeneralizedpooling_pa_e_kernel(
         hidden(last, 1)
         second_matmul_chunk(first // 2 - 1)
         weighted_sums(first - 3)
+        invert_heads()
         hidden(last, 2)
         add_mask(first - 2)
         hidden(last, 3)
         quantise_block(0)
+        divide_heads()
         second_matmul_sentence(first)
         second_matmul_block(0)
         add_mask(first - 1)
@@ -607,18 +624,17 @@ def tile_multiheadgeneralizedpooling_pa_e_kernel(
         products(first - 2)
         add_mask(first)
         add_mask_block(0)
-        sums(first - 2)
         find_max(first)
         exponentials(first)
-        find_max_block(0)
         products(first - 1)
+        invert_chunk()
+        sums(first - 2)
         add_mask_block(1)
-        invert_all()
+        find_max_block(0)
+        invert(first)
         find_max_block(1)
         exponentials(last)
-        divide_all()
         sums(first - 1)
-        invert(first)
         weighted_sums(first, (0,))
         invert(last, (0,))
         weighted_sums(first, (1,))

@@ -33,7 +33,7 @@ AHEAD = 3
 
 WARM = 6
 INTERLEAVE = True
-V_LATE = (9, 12, 15)
+V_LATE = (9, 12)
 V_COPIES = 3
 MX_BATCH = True
 NO_TR_BEFORE_MX = True
@@ -113,16 +113,23 @@ def tile_multiheadgeneralizedpooling_pa_e_kernel(
                 return w1_sb, w1T, head, half
             return h_sb, hT, head, half
 
+        def load_h(head, n):
+            together = 1 if (head, n) == (0, 0) else SENTENCES
+            rows = h_heads[head].rearrange("b (p j) f -> p b j f", p=P)
+            tile = h_sb[head][n][:].rearrange("p (b j) f -> p b j f", b=SENTENCES)
+            for s in range(0, SENTENCES, together):
+                first = n * SENTENCES + s
+                nc.sync.dma_start(out=tile[:, s : s + together], in_=rows[:, first : first + together])
+
         def load_quarter(j):
             source, unused, head, half = quarter_of(j)
             if j % 2 == 0:
                 rows = W1[head].rearrange("(g p t) f -> p g t f", g=PASSES, p=P, t=PACK)
             else:
-                rows = h_heads[head].flatten_outer_dims().rearrange(
-                    "(n j p) f -> p n j f", n=CHUNKS, j=BLOCKS, p=P
-                )
+                load_h(head, half)
+                return
             pieces = FIRST_PIECES[j] if j < FIRST_QUARTERS else 1
-            width = BLOCKS // pieces
+            width = PACK // pieces
             for i in range(pieces):
                 part = slice(i * width, (i + 1) * width)
                 nc.sync.dma_start(out=source[head][half][:, part, :], in_=rows[:, half][:, part, :])
@@ -173,7 +180,11 @@ def tile_multiheadgeneralizedpooling_pa_e_kernel(
                 nc.tensor.matmul(
                     spread[:], lhsT=ones[:], rhs=mask_row[:, tokens], start=True, stop=True
                 )
-                nc.scalar.activation(out=log_mask[:, tokens], in_=spread[:], func=ACT.Ln)
+                nc.scalar.activation(
+                    out=log_mask[:, tokens].rearrange("p (s j q) -> p s j q", s=SENTENCES, q=P),
+                    in_=spread[:].rearrange("p (s q j) -> p s j q", s=SENTENCES, q=P),
+                    func=ACT.Ln,
+                )
             nc.scalar.activation(out=table_warmer[:, 1:2], in_=table_warmer[:, 0:1], func=ACT.Exp)
 
         def open_quarter(j):

@@ -31,7 +31,8 @@ QUARTERS = NH * 4
 FIRST_QUARTERS = 2
 AHEAD = 3
 
-WARM = 6
+WARM_F32 = 2
+WARM = 4
 INTERLEAVE = True
 V_LATE = (9, 12)
 V_COPIES = 3
@@ -90,13 +91,14 @@ def tile_multiheadgeneralizedpooling_pa_e_kernel(
             [keep.tile([P, PACK, F_TILES, P], BF16, name="w1T_%d_%d" % (i, g)) for g in range(PASSES)]
             for i in range(NH)
         ]
-        bias = keep.tile([P, NH, PASSES, PACK], BF16)
+        bias = [keep.tile([P, PASSES, PACK], BF16, name="bias_%d" % i) for i in range(NH)]
         w2_words = [
             keep.tile([P, PASSES, HD], U32, name="w2_words_%d" % i, align_bytes=64) for i in range(NH)
         ]
         w2_scales = keep.tile([P, NH * PASSES, HD], U8, align_bytes=64)
         mask_row = keep.tile([P, TOKENS], BF16)
         ones = keep.tile([P, P], BF16)
+        ones_f32 = keep.tile([P, P], F32)
         log_mask = keep.tile([P, TOKENS], F32)
         ident_bf = keep.tile([P, P], BF16)
         ident_f32 = keep.tile([P, P], F32)
@@ -145,31 +147,40 @@ def tile_multiheadgeneralizedpooling_pa_e_kernel(
         make_identity(nc, ident_bf[:])
         make_identity(nc, ident_f32[:])
         nc.vector.memset(ones[:], 1.0)
+        nc.vector.memset(ones_f32[:], 1.0)
         nc.vector.memset(mask_row[:].bitcast(I32), 0)
         nc.vector.memset(table_warmer[:], 1.0)
         nc.vector.memset(w2_scales[:].rearrange("p g n -> p (g n)").bitcast(I32), 0)
         nc.vector.memset(pooled[:], 0.0)
-        for head in range(NH):
-            for j in (list(FIRST_ORDER) + [2, 3] if head == 0 else range(4 * head, 4 * head + 4)):
-                load_quarter(j)
-                if j == FIRST_ORDER[-1]:
-                    nc.sync.dma_start(
-                        out=mask_row[0:1, :],
-                        in_=attention_mask.rearrange("b s -> (b s)").unsqueeze(0),
-                    )
-                    nc.sync.dma_start(
-                        out=bias[:],
-                        in_=b1.rearrange("i (g p t) -> p i g t", g=PASSES, p=P, t=PACK),
-                    )
-            if head == 0:
-                for quadrant in range(4):
-                    nc.sync.dma_start(
-                        out=w2_scales[32 * quadrant : 32 * quadrant + 4, :, :].bitcast(I32),
-                        in_=W2_scales.bitcast(I32)[
-                            :, 4 * quadrant : 4 * quadrant + 4, :
-                        ].rearrange("g r n -> r g n"),
-                    )
-            load_w2_words(head)
+        def load_bias(head):
+            nc.sync.dma_start(
+                out=bias[head][:], in_=b1[head].rearrange("(g p t) -> p g t", g=PASSES, p=P, t=PACK)
+            )
+
+        def load_scales():
+            for quadrant in range(4):
+                nc.sync.dma_start(
+                    out=w2_scales[32 * quadrant : 32 * quadrant + 4, :, :].bitcast(I32),
+                    in_=W2_scales.bitcast(I32)[
+                        :, 4 * quadrant : 4 * quadrant + 4, :
+                    ].rearrange("g r n -> r g n"),
+                )
+
+        for j in FIRST_ORDER:
+            load_quarter(j)
+        nc.sync.dma_start(
+            out=mask_row[0:1, :], in_=attention_mask.rearrange("b s -> (b s)").unsqueeze(0)
+        )
+        load_bias(0)
+        for j in range(FIRST_QUARTERS, QUARTERS):
+            load_quarter(j)
+            head = j // 4
+            if j % 4 == 0:
+                load_bias(head)
+                if head == 1:
+                    load_scales()
+                load_w2_words(head - 1)
+        load_w2_words(NH - 1)
 
         nc.scalar.activation(out=table_warmer[:, 1:2], in_=table_warmer[:, 0:1], func=ACT.Ln)
 
@@ -249,7 +260,7 @@ def tile_multiheadgeneralizedpooling_pa_e_kernel(
                 nc.vector.tensor_scalar(
                     out=by_t[u][:, t, :],
                     in0=pre[:],
-                    scalar1=bias[:, head, g, t : t + 1],
+                    scalar1=bias[head][:, g, t : t + 1],
                     scalar2=0.0,
                     op0=ALU.add,
                     op1=ALU.max,
@@ -259,7 +270,7 @@ def tile_multiheadgeneralizedpooling_pa_e_kernel(
                 out=by_t[u][:, t, :],
                 in_=pre[:],
                 func=ACT.Relu,
-                bias=bias[:, head, g, t : t + 1],
+                bias=bias[head][:, g, t : t + 1],
                 scale=1.0,
             )
 
@@ -277,7 +288,7 @@ def tile_multiheadgeneralizedpooling_pa_e_kernel(
             nc.tensor.matmul(
                 pre[:],
                 lhsT=ident_bf[:],
-                rhs=bias[:, head, g, :].unsqueeze(2).to_broadcast([P, PACK, P]),
+                rhs=bias[head][:, g, :].unsqueeze(2).to_broadcast([P, PACK, P]),
                 start=True,
                 stop=False,
             )
@@ -531,10 +542,10 @@ def tile_multiheadgeneralizedpooling_pa_e_kernel(
                     accum_out=(pooled if r >= FIRST_SCALED else num)[:, column],
                 )
 
-        if WARM:
-            junk = psum_work.tile([P, CHUNK], F32, tag="bank")
-            for i in range(WARM):
-                nc.tensor.matmul(junk[:, 0:P], lhsT=ones[:], rhs=ones[:], start=True, stop=True)
+        junk = psum_work.tile([P, CHUNK], F32, tag="bank")
+        for operand, passes in ((ones, WARM), (ones_f32, WARM_F32)):
+            for i in range(passes):
+                nc.tensor.matmul(junk[:, 0:P], lhsT=operand[:], rhs=operand[:], start=True, stop=True)
         def first_piece(j, part, pool, tag, copy, plain=False):
             source, transposed, head, half = quarter_of(j)
             width = part.stop - part.start

from contextlib import ExitStack

import concourse.mybir as mybir
from concourse.masks import make_identity

BF16 = mybir.dt.bfloat16
F32 = mybir.dt.float32
I32 = mybir.dt.int32
U32 = mybir.dt.uint32
U8 = mybir.dt.uint8
FP8X4 = mybir.dt.float8_e4m3fn_x4
ACT = mybir.ActivationFunctionType
ALU = mybir.AluOpType
AXIS = mybir.AxisListType

P = 128
NH, B, S, HD, HID = 4, 4, 256, 256, 1024
PACK = 4
K_PASS = P * PACK
PASSES = HID // K_PASS
F_TILES = HD // P
TOKENS = B * S
CHUNK = 512
CHUNKS = TOKENS // CHUNK
SENTENCES = CHUNK // S
BLOCKS = CHUNK // P

GROUPS = NH * CHUNKS * PASSES
HALVES = NH * CHUNKS * F_TILES
QUARTERS = NH * 4
FIRST_QUARTERS = 2
AHEAD = 3

WARM_F32 = 2
WARM = 4
INTERLEAVE = True
V_LATE = (9, 12)
V_COPIES = 3
MX_BATCH = True
NO_TR_BEFORE_MX = True
MX_POS = 2
EXP_POS = 2
V_GROUPS = 1


LAST = GROUPS - 1
FIRST_SCALED = HALVES - 4
LAST_GROUPS = (GROUPS - 2, LAST)
PE_FROM = 6
FIRST_PIECES = (2, 2)
FIRST_ORDER = (1, 0)
PE_EVERY = 3


def by_sentence(u):
    return u in LAST_GROUPS


def bias_on_tensor(u):
    return by_sentence(u) or (u >= PE_FROM and u % PE_EVERY == 0)

FLOPS = 2 * 2 * NH * TOKENS * HID * HD


def tile_multiheadgeneralizedpooling_pa_e_kernel(
    tc, h_heads, attention_mask, W1, b1, W2_words, W2_scales, out
):
    nc = tc.nc
    with ExitStack() as ctx:
        ctx.enter_context(tc.manual_schedule())
        keep = ctx.enter_context(tc.tile_pool(name="keep", bufs=1))
        hid_pool = ctx.enter_context(tc.tile_pool(name="hid", bufs=4))
        soft_pool = ctx.enter_context(tc.tile_pool(name="soft", bufs=6))
        psum_work = ctx.enter_context(tc.psum_pool(name="psum_work", bufs=4 if INTERLEAVE else 6))
        psum_tp = ctx.enter_context(tc.psum_pool(name="psum_tp", bufs=2)) if INTERLEAVE else psum_work
        psum_att = ctx.enter_context(tc.psum_pool(name="psum_att", bufs=2))

        h_sb = [
            [keep.tile([P, BLOCKS, HD], BF16, name="h_sb_%d_%d" % (i, n)) for n in range(CHUNKS)]
            for i in range(NH)
        ]
        w1_sb = [
            [keep.tile([P, PACK, HD], BF16, name="w1_sb_%d_%d" % (i, g)) for g in range(PASSES)]
            for i in range(NH)
        ]
        hT = [
            [keep.tile([P, F_TILES, BLOCKS, P], BF16, name="hT_%d_%d" % (i, n)) for n in range(CHUNKS)]
            for i in range(NH)
        ]
        w1T = [
            [keep.tile([P, PACK, F_TILES, P], BF16, name="w1T_%d_%d" % (i, g)) for g in range(PASSES)]
            for i in range(NH)
        ]
        bias = [keep.tile([P, PASSES, PACK], BF16, name="bias_%d" % i) for i in range(NH)]
        w2_words = [
            keep.tile([P, PASSES, HD], U32, name="w2_words_%d" % i, align_bytes=64) for i in range(NH)
        ]
        w2_scales = keep.tile([P, NH * PASSES, HD], U8, align_bytes=64)
        mask_row = keep.tile([P, TOKENS], BF16)
        ones = keep.tile([P, P], BF16)
        ones_f32 = keep.tile([P, P], F32)
        log_mask = keep.tile([P, TOKENS], F32)
        ident_bf = keep.tile([P, P], BF16)
        ident_f32 = keep.tile([P, P], F32)
        columns = B * NH * F_TILES
        den = keep.tile([P, columns], F32)
        num = keep.tile([P, columns], F32)
        inv_den = keep.tile([P, columns], F32)
        pooled = keep.tile([P, P], F32)
        table_warmer = keep.tile([P, 2], F32)

        def quarter_of(j):
            head, half = j // 4, (j % 4) // 2
            if j % 2 == 0:
                return w1_sb, w1T, head, half
            return h_sb, hT, head, half

        def load_h(head, n):
            together = 1 if (head, n) == (0, 0) else SENTENCES
            rows = h_heads[head].rearrange("b (p j) f -> p b j f", p=P)
            tile = h_sb[head][n][:].rearrange("p (b j) f -> p b j f", b=SENTENCES)
            for s in range(0, SENTENCES, together):
                first = n * SENTENCES + s
                nc.sync.dma_start(out=tile[:, s : s + together], in_=rows[:, first : first + together])

        def load_quarter(j):
            source, unused, head, half = quarter_of(j)
            if j % 2 == 0:
                rows = W1[head].rearrange("(g p t) f -> p g t f", g=PASSES, p=P, t=PACK)
            else:
                load_h(head, half)
                return
            pieces = FIRST_PIECES[j] if j < FIRST_QUARTERS else 1
            width = PACK // pieces
            for i in range(pieces):
                part = slice(i * width, (i + 1) * width)
                nc.sync.dma_start(out=source[head][half][:, part, :], in_=rows[:, half][:, part, :])

        def load_w2_words(head):
            rows = slice(head * PASSES, (head + 1) * PASSES)
            words = W2_words.rearrange("g p n t -> g p (n t)").bitcast(I32)
            nc.sync.dma_start(
                out=w2_words[head][:].bitcast(I32),
                in_=words[rows].rearrange("g p n -> p g n"),
            )

        make_identity(nc, ident_bf[:])
        make_identity(nc, ident_f32[:])
        nc.vector.memset(ones[:], 1.0)
        nc.vector.memset(ones_f32[:], 1.0)
        nc.vector.memset(mask_row[:].bitcast(I32), 0)
        nc.vector.memset(table_warmer[:], 1.0)
        nc.vector.memset(w2_scales[:].rearrange("p g n -> p (g n)").bitcast(I32), 0)
        nc.vector.memset(pooled[:], 0.0)
        def load_bias(head):
            nc.sync.dma_start(
                out=bias[head][:], in_=b1[head].rearrange("(g p t) -> p g t", g=PASSES, p=P, t=PACK)
            )

        def load_scales():
            for quadrant in range(4):
                nc.sync.dma_start(
                    out=w2_scales[32 * quadrant : 32 * quadrant + 4, :, :].bitcast(I32),
                    in_=W2_scales.bitcast(I32)[
                        :, 4 * quadrant : 4 * quadrant + 4, :
                    ].rearrange("g r n -> r g n"),
                )

        for j in FIRST_ORDER:
            load_quarter(j)
        nc.sync.dma_start(
            out=mask_row[0:1, :], in_=attention_mask.rearrange("b s -> (b s)").unsqueeze(0)
        )
        load_bias(0)
        for j in range(FIRST_QUARTERS, QUARTERS):
            load_quarter(j)
            head = j // 4
            if j % 4 == 0:
                load_bias(head)
                if head == 1:
                    load_scales()
                load_w2_words(head - 1)
        load_w2_words(NH - 1)

        nc.scalar.activation(out=table_warmer[:, 1:2], in_=table_warmer[:, 0:1], func=ACT.Ln)

        def log_of_mask():
            for n in range(CHUNKS):
                tokens = slice(n * CHUNK, (n + 1) * CHUNK)
                spread = psum_work.tile([P, CHUNK], F32, tag="bank")
                nc.tensor.matmul(
                    spread[:], lhsT=ones[:], rhs=mask_row[:, tokens], start=True, stop=True
                )
                nc.scalar.activation(
                    out=log_mask[:, tokens].rearrange("p (s j q) -> p s j q", s=SENTENCES, q=P),
                    in_=spread[:].rearrange("p (s q j) -> p s j q", s=SENTENCES, q=P),
                    func=ACT.Ln,
                )
            nc.scalar.activation(out=table_warmer[:, 1:2], in_=table_warmer[:, 0:1], func=ACT.Exp)

        def open_quarter(j):
            source, transposed, head, half = quarter_of(j)
            if j % 2 == 0:
                tp = psum_tp.tile([P, PACK, F_TILES, P], BF16, name="tp", tag="tp")
                slots = [(x, c, tp[:, x, c, :]) for x in range(PACK) for c in range(F_TILES)]
            else:
                tp = psum_tp.tile([P, F_TILES, BLOCKS, P], BF16, name="tp", tag="tp")
                slots = [(x, c, tp[:, c, x, :]) for x in range(BLOCKS) for c in range(F_TILES)]
            pairs = [(slot, source[head][half][:, x, c * P : (c + 1) * P]) for x, c, slot in slots]
            return tp, pairs

        def transpose_quarter(j):
            tp, pairs = open_quarter(j)
            for target, block in pairs:
                nc.tensor.transpose(target, block, ident_bf[:])
            copy_quarter(j, tp)

        def copy_quarter(j, tp):
            source, transposed, head, half = quarter_of(j)
            words_in = tp[:].rearrange("p c x q -> p c (x q)").bitcast(F32)
            words_out = transposed[head][half][:].rearrange("p c x q -> p c (x q)").bitcast(F32)
            if j < V_COPIES or j in V_LATE:
                nc.vector.tensor_copy(out=words_out, in_=words_in)
            else:
                nc.scalar.copy(out=words_out, in_=words_in)

        by_t = {}
        grouped = {}
        codes = {}
        scales = {}
        att = {}
        score = {}
        neg_max = {}
        product = {}
        weight = {}

        def hidden(u, t, woven=(), end_plain=False):
            head, n, g = u // 4, (u // 2) % 2, u % 2
            if bias_on_tensor(u):
                hidden_block(u, t, woven, end_plain)
                return
            if t == 0:
                by_t[u] = hid_pool.tile([P, PACK, CHUNK], BF16, name="by_t", tag="by_t")
            pre = psum_work.tile([P, CHUNK], F32, tag="bank")
            for c in range(F_TILES):
                nc.tensor.matmul(
                    pre[:],
                    lhsT=w1T[head][g][:, t, c, :],
                    rhs=hT[head][n][:, c].rearrange("p j x -> p (j x)"),
                    start=(c == 0),
                    stop=(c == F_TILES - 1),
                )
                share = len(woven) // F_TILES
                mine = woven[c * share : (c + 1) * share]
                if end_plain:
                    mine = woven if c == 0 else ()
                for target, block in mine:
                    nc.tensor.transpose(target, block, ident_bf[:])
            if u < V_GROUPS:
                nc.vector.tensor_scalar(
                    out=by_t[u][:, t, :],
                    in0=pre[:],
                    scalar1=bias[head][:, g, t : t + 1],
                    scalar2=0.0,
                    op0=ALU.add,
                    op1=ALU.max,
                )
                return
            nc.scalar.activation(
                out=by_t[u][:, t, :],
                in_=pre[:],
                func=ACT.Relu,
                bias=bias[head][:, g, t : t + 1],
                scale=1.0,
            )

        def hidden_block(u, j, woven, end_plain=False):
            head, n, g = u // 4, (u // 2) % 2, u % 2
            slot = j
            if by_sentence(u):
                x, g = (slot // 2, slot % 2) if u == LAST else (slot % 2, slot // 2)
                j = (S // P) * (u % 2) + x
            if slot == 0:
                grouped[u] = hid_pool.tile(
                    [P, CHUNK, PACK], BF16, name="grouped", tag="grouped", align_bytes=64
                )
            pre = psum_work.tile([P, PACK, P], F32, tag="bank")
            nc.tensor.matmul(
                pre[:],
                lhsT=ident_bf[:],
                rhs=bias[head][:, g, :].unsqueeze(2).to_broadcast([P, PACK, P]),
                start=True,
                stop=False,
            )
            for t in range(PACK):
                for c in range(F_TILES):
                    nc.tensor.matmul(
                        pre[:, t, :],
                        lhsT=w1T[head][g][:, t, c, :],
                        rhs=hT[head][n][:, c, j, :],
                        start=False,
                        stop=(t == PACK - 1 and c == F_TILES - 1),
                    )
                if t % 2 == (0 if end_plain else 1):
                    for target, block in woven[t // 2 : t // 2 + 1]:
                        nc.tensor.transpose(target, block, ident_bf[:])
            nc.scalar.activation(
                out=grouped[u][:, slot * P : (slot + 1) * P, :],
                in_=pre[:].rearrange("p t x -> p x t"),
                func=ACT.Relu,
            )

        def regroup(u):
            if bias_on_tensor(u):
                return
            grouped[u] = hid_pool.tile(
                [P, CHUNK, PACK], BF16, name="grouped", tag="grouped", align_bytes=64
            )
            nc.vector.tensor_copy(
                out=grouped[u][:].rearrange("p (w r) t -> p w t r", r=8),
                in_=by_t[u][:].rearrange("p t (w r) -> p w t r", r=8),
            )

        def quantise(u):
            codes[u] = hid_pool.tile([P, CHUNK], U32, name="codes", tag="codes", align_bytes=64)
            scales[u] = hid_pool.tile([P, CHUNK], U8, name="scales", tag="scales", align_bytes=64)
            nc.vector.quantize_mx(
                out=codes[u][:].bitcast(FP8X4),
                scales=scales[u][:],
                in_=grouped[u][:].rearrange("p w t -> p (w t)"),
            )

        def second_matmul(u):
            g = u % 2
            for m in range(F_TILES):
                r = (u // 2) * F_TILES + m
                if g == 0:
                    att[r] = psum_att.tile([P, CHUNK], F32, name="att", tag="att")
                features = slice(m * P, (m + 1) * P)
                nc.tensor.matmul_mx(
                    out=att[r][:],
                    lhsT=w2_words[u // 4][:, g, features].bitcast(FP8X4),
                    lhsT_scale=w2_scales[:, (u // 4) * PASSES + g, features],
                    rhs=codes[u][:].bitcast(FP8X4),
                    rhs_scale=scales[u][:],
                    start=(g == 0),
                    stop=(g == PASSES - 1),
                )

        def second_matmul_chunk(chunk):
            for m in range(F_TILES):
                r = chunk * F_TILES + m
                att[r] = psum_att.tile([P, CHUNK], F32, name="att", tag="att")
                features = slice(m * P, (m + 1) * P)
                for g in range(PASSES):
                    u = chunk * PASSES + g
                    nc.tensor.matmul_mx(
                        out=att[r][:],
                        lhsT=w2_words[u // 4][:, g, features].bitcast(FP8X4),
                        lhsT_scale=w2_scales[:, (u // 4) * PASSES + g, features],
                        rhs=codes[u][:].bitcast(FP8X4),
                        rhs_scale=scales[u][:],
                        start=(g == 0),
                        stop=(g == PASSES - 1),
                    )

        def second_matmul_sentence(u):
            att[u] = psum_tp.tile([P, F_TILES, S], F32, name="tp", tag="tp")
            for m in range(F_TILES):
                features = slice(m * P, (m + 1) * P)
                for g in range(PASSES):
                    nc.tensor.matmul_mx(
                        out=att[u][:, m, :],
                        lhsT=w2_words[u // 4][:, g, features].bitcast(FP8X4),
                        lhsT_scale=w2_scales[:, (u // 4) * PASSES + g, features],
                        rhs=codes[u][:, g * S : (g + 1) * S].bitcast(FP8X4),
                        rhs_scale=scales[u][:, g * S : (g + 1) * S],
                        start=(g == 0),
                        stop=(g == PASSES - 1),
                    )

        def quantise_block(x):
            u = LAST
            width = PASSES * P
            codes[u, x] = hid_pool.tile([P, width], U32, name="codes", tag="codes", align_bytes=64)
            scales[u, x] = hid_pool.tile([P, width], U8, name="scales", tag="scales", align_bytes=64)
            nc.vector.quantize_mx(
                out=codes[u, x][:].bitcast(FP8X4),
                scales=scales[u, x][:],
                in_=grouped[u][:, x * width : (x + 1) * width, :].rearrange("p w t -> p (w t)"),
            )

        def second_matmul_block(x):
            u = LAST
            pool, tag = ((psum_tp, "tp"), (psum_att, "att"))[x]
            att[u, x] = pool.tile([P, F_TILES, P], F32, name="att_block", tag=tag)
            for m in range(F_TILES):
                features = slice(m * P, (m + 1) * P)
                for g in range(PASSES):
                    nc.tensor.matmul_mx(
                        out=att[u, x][:, m, :],
                        lhsT=w2_words[u // 4][:, g, features].bitcast(FP8X4),
                        lhsT_scale=w2_scales[:, (u // 4) * PASSES + g, features],
                        rhs=codes[u, x][:, g * P : (g + 1) * P].bitcast(FP8X4),
                        rhs_scale=scales[u, x][:, g * P : (g + 1) * P],
                        start=(g == 0),
                        stop=(g == PASSES - 1),
                    )

        def add_mask_block(x):
            if x == 0:
                score[LAST] = soft_pool.tile([P, F_TILES, S + 1], F32, name="score", tag="score_last")
            first = TOKENS - S + x * P
            nc.vector.tensor_tensor(
                out=score[LAST][:, :, x * P : (x + 1) * P],
                in0=att[LAST, x][:],
                in1=log_mask[:, first : first + P].unsqueeze(1).to_broadcast([P, F_TILES, P]),
                op=ALU.add,
            )

        def find_max_block(x):
            if x == 0:
                nc.vector.tensor_reduce(
                    out=score[LAST][:, :, S], in_=score[LAST][:, :, 0:P], axis=AXIS.X, op=ALU.max
                )
                return
            neg_max[LAST] = soft_pool.tile([P, SENTENCES], F32, name="neg_max", tag="neg_max")
            nc.vector.tensor_reduce(
                out=neg_max[LAST][:], in_=score[LAST][:, :, P : S + 1], axis=AXIS.X, op=ALU.max, negate=True
            )

        def products(r):
            head, n, m = r // (CHUNKS * F_TILES), (r // F_TILES) % CHUNKS, r % F_TILES
            per_sentence = S // P
            for s in range(SENTENCES):
                tile_m, sent = (s, m) if by_sentence(r) else (m, s)
                product[r, s] = soft_pool.tile([P, S], F32, name="product", tag="product")
                nc.gpsimd.tensor_tensor(
                    out=product[r, s][:],
                    in0=weight[r, s][:],
                    in1=hT[head][n][:, tile_m, sent * per_sentence : (sent + 1) * per_sentence, :].rearrange(
                        "p j x -> p (j x)"
                    ),
                    op=ALU.mult,
                )

        def sums(r):
            for s in range(SENTENCES):
                column = slice(column_of(r, s), column_of(r, s) + 1)
                nc.scalar.activation(
                    out=weight[r, s][:],
                    in_=product[r, s][:],
                    func=ACT.Copy,
                    scale=inv_den[:, column] if r >= FIRST_SCALED else 1.0,
                    accum_out=(pooled if r >= FIRST_SCALED else num)[:, column],
                )

        def add_mask(r):
            n = (r // F_TILES) % CHUNKS
            score[r] = soft_pool.tile([P, SENTENCES, S], F32, name="score", tag="score")
            if by_sentence(r):
                first = n * CHUNK + (r % 2) * S
                nc.vector.tensor_tensor(
                    out=score[r][:],
                    in0=att[r][:],
                    in1=log_mask[:, first : first + S].unsqueeze(1).to_broadcast([P, F_TILES, S]),
                    op=ALU.add,
                )
                return
            nc.vector.tensor_tensor(
                out=score[r][:].rearrange("p b s -> p (b s)"),
                in0=att[r][:],
                in1=log_mask[:, n * CHUNK : (n + 1) * CHUNK],
                op=ALU.add,
            )

        def find_max(r):
            neg_max[r] = soft_pool.tile([P, SENTENCES], F32, name="neg_max", tag="neg_max")
            nc.vector.tensor_reduce(
                out=neg_max[r][:], in_=score[r][:], axis=AXIS.X, op=ALU.max, negate=True
            )

        def column_of(r, s):
            head, n, m = r // (CHUNKS * F_TILES), (r // F_TILES) % CHUNKS, r % F_TILES
            if by_sentence(r):
                m, s = s, m
            return ((n * SENTENCES + s) * NH + head) * F_TILES + m

        def exponentials(r):
            for s in range(SENTENCES):
                weight[r, s] = soft_pool.tile([P, S], F32, name="weight", tag="weight")
                nc.scalar.activation(
                    out=weight[r, s][:],
                    in_=score[r][:, s, 0:S],
                    func=ACT.Exp,
                    bias=neg_max[r][:, s : s + 1],
                    scale=1.0,
                    accum_out=den[:, column_of(r, s) : column_of(r, s) + 1],
                )

        def by_row(tile):
            return tile[:, 0:columns].rearrange("p (b c) -> p b c", b=B)

        whole_heads = slice(0, (NH - 1) * F_TILES)

        def invert_heads():
            nc.vector.reciprocal(out=by_row(inv_den)[:, :, whole_heads], in_=by_row(den)[:, :, whole_heads])

        def divide_heads():
            nc.vector.tensor_tensor(
                out=by_row(pooled)[:, :, whole_heads],
                in0=by_row(num)[:, :, whole_heads],
                in1=by_row(inv_den)[:, :, whole_heads],
                op=ALU.mult,
            )

        def invert_chunk():
            part = (slice(None), slice(0, SENTENCES), slice((NH - 1) * F_TILES, NH * F_TILES))
            nc.vector.reciprocal(out=by_row(inv_den)[part], in_=by_row(den)[part])

        def invert(r, which=tuple(range(SENTENCES))):
            cols = [column_of(r, s) for s in which]
            part = slice(cols[0], cols[-1] + 1, max(cols[-1] - cols[0], 1))
            nc.vector.reciprocal(out=inv_den[:, part], in_=den[:, part])

        def weighted_sums(r, which=tuple(range(SENTENCES))):
            head, n, m = r // (CHUNKS * F_TILES), (r // F_TILES) % CHUNKS, r % F_TILES
            per_sentence = S // P
            for s in which:
                weighted = soft_pool.tile([P, S], F32, tag="weighted")
                tile_m, sent = (s, m) if by_sentence(r) else (m, s)
                column = slice(column_of(r, s), column_of(r, s) + 1)
                nc.vector.scalar_tensor_tensor(
                    out=weighted[:],
                    in0=weight[r, s][:],
                    scalar=inv_den[:, column] if r >= FIRST_SCALED else 1.0,
                    in1=hT[head][n][:, tile_m, sent * per_sentence : (sent + 1) * per_sentence, :].rearrange(
                        "p j x -> p (j x)"
                    ),
                    op0=ALU.mult,
                    op1=ALU.mult,
                    accum_out=(pooled if r >= FIRST_SCALED else num)[:, column],
                )

        junk = psum_work.tile([P, CHUNK], F32, tag="bank")
        for operand, passes in ((ones, WARM), (ones_f32, WARM_F32)):
            for i in range(passes):
                nc.tensor.matmul(junk[:, 0:P], lhsT=operand[:], rhs=operand[:], start=True, stop=True)
        def first_piece(j, part, pool, tag, copy, plain=False):
            source, transposed, head, half = quarter_of(j)
            width = part.stop - part.start
            if j % 2 == 0:
                tp = pool.tile([P, width, F_TILES, P], BF16, name="first", tag=tag)
                target = transposed[head][half][:, part].rearrange("p x c q -> p (x c q)")
                words_in = tp[:].rearrange("p x c q -> p (x c q)").bitcast(F32)
                slots = [(x, c, tp[:, x, c, :]) for x in range(width) for c in range(F_TILES)]
                words_out = target.bitcast(F32)
            else:
                tp = pool.tile([P, F_TILES, width, P], BF16, name="first", tag=tag)
                slots = [(x, c, tp[:, c, x, :]) for x in range(width) for c in range(F_TILES)]
                words_in = tp[:].rearrange("p c x q -> p c (x q)").bitcast(F32)
                words_out = transposed[head][half][:, :, part].rearrange("p c x q -> p c (x q)").bitcast(F32)
            for x, c, slot in slots:
                block = source[head][half][:, part.start + x, c * P : (c + 1) * P]
                if plain:
                    nc.tensor.matmul(slot, lhsT=block, rhs=ident_bf[:], start=True, stop=True)
                else:
                    nc.tensor.transpose(slot, block, ident_bf[:])
            copy(out=words_out, in_=words_in)

        first_piece(1, slice(0, 2), psum_att, "att", nc.vector.tensor_copy, True)
        first_piece(1, slice(2, 4), psum_att, "att", nc.vector.tensor_copy, True)
        first_piece(0, slice(0, 2), psum_tp, "tp", nc.scalar.copy)
        first_piece(0, slice(2, 4), psum_tp, "tp", nc.scalar.copy)
        log_of_mask()
        late = []
        for k in range(GROUPS - 1):
            first_quarter = FIRST_QUARTERS if k == 0 else k + AHEAD
            quarters = list(range(first_quarter, min(k + AHEAD + 1, QUARTERS)))
            opened = [(j, open_quarter(j)) for j in quarters] if INTERLEAVE else []
            woven = [pair for j, (tp, pairs) in opened for pair in pairs]
            share = len(woven) // PACK
            banks_each = PACK // max(len(opened), 1)
            for t in range(PACK + 1):
                mx_here = 0 <= k - 2 < GROUPS and (k % 2 == 1 or not MX_BATCH)
                if t == MX_POS and mx_here:
                    if MX_BATCH:
                        second_matmul_chunk((k - 3) // 2)
                    else:
                        second_matmul(k - 2)
                if t == EXP_POS and 0 <= k - 4 < HALVES:
                    exponentials(k - 4)
                if t < PACK and k < GROUPS:
                    hidden(k, t, woven[t * share : (t + 1) * share], NO_TR_BEFORE_MX and mx_here and t + 1 == MX_POS)
                    if opened and (t + 1) % banks_each == 0:
                        j, (tp, pairs) = opened[t // banks_each]
                        if j in V_LATE:
                            late.append((j, tp))
                        else:
                            copy_quarter(j, tp)
            if not INTERLEAVE:
                for j in quarters:
                    transpose_quarter(j)
            chunk = (k - 3) // 2
            has_chunk = 0 <= chunk < NH * CHUNKS
            scores_complete = has_chunk and k % 2 == 1
            if 0 <= k - 1 < GROUPS:
                regroup(k - 1)
            if late and late[0][0] == k - 1 + AHEAD:
                copy_quarter(*late.pop())
            if scores_complete:
                add_mask(chunk * F_TILES)
            if has_chunk and not scores_complete:
                find_max(chunk * F_TILES + 1)
            if 0 <= k - 1 < GROUPS:
                quantise(k - 1)
            if scores_complete:
                add_mask(chunk * F_TILES + 1)
            if scores_complete:
                find_max(chunk * F_TILES)
            if 0 <= k - 4 < HALVES:
                weighted_sums(k - 4)

        first, last = LAST_GROUPS
        quantise(first)
        exponentials(first - 3)
        hidden(last, 0)
        hidden(last, 1)
        second_matmul_chunk(first // 2 - 1)
        weighted_sums(first - 3)
        invert_heads()
        hidden(last, 2)
        add_mask(first - 2)
        hidden(last, 3)
        quantise_block(0)
        divide_heads()
        second_matmul_sentence(first)
        second_matmul_block(0)
        add_mask(first - 1)
        find_max(first - 2)
        find_max(first - 1)
        quantise_block(1)
        second_matmul_block(1)
        exponentials(first - 2)
        exponentials(first - 1)
        products(first - 2)
        add_mask(first)
        add_mask_block(0)
        find_max(first)
        exponentials(first)
        products(first - 1)
        invert_chunk()
        sums(first - 2)
        add_mask_block(1)
        find_max_block(0)
        invert(first)
        find_max_block(1)
        exponentials(last)
        sums(first - 1)
        weighted_sums(first, (0,))
        invert(last, (0,))
        weighted_sums(first, (1,))
        invert(last, (1,))
        weighted_sums(last)

        pooledT = psum_work.tile([P, P], F32, tag="bank")
        nc.tensor.transpose(pooledT[:], pooled[:], ident_f32[:])
        result = keep.tile([columns, P], F32)
        nc.vector.tensor_copy(out=result[:], in_=pooledT[0:columns, :])
        nc.sync.dma_start(out=out.rearrange("b (r f) -> (b r) f", f=P), in_=result[:])
